import numpy as np
import ml_dtypes


def mxq(x, axis, fmt="e4m3"):
    dtype, down = {"e4m3": (ml_dtypes.float8_e4m3fn, 7), "e5m2": (ml_dtypes.float8_e5m2, 14)}[fmt]
    v = np.moveaxis(np.asarray(x, np.float32).astype(ml_dtypes.bfloat16).astype(np.float64), axis, -1)
    blocks = v.reshape(v.shape[:-1] + (-1, 32))
    amax = np.abs(blocks).max(-1, keepdims=True)
    byte = np.maximum(np.where(amax > 0, np.frexp(amax)[1] - 1 + 127, 0) - down, 1)
    scale = np.exp2(byte - 127.0)
    codes = (blocks / scale).astype(np.float32).astype(dtype).astype(np.float64)
    return np.moveaxis((codes * scale).reshape(v.shape), -1, axis)


WIDE = False


def mx_kscale(k):
    if not WIDE:
        return np.ones(k)
    levels = np.array([10, -10, 5, -5, 0])
    a = np.random.permutation(np.resize(levels, k // 512 * 4)).reshape(k // 512, 4)
    idx = np.arange(k)
    return np.exp2(a[idx // 512, idx % 128 // 32])


BF16 = ml_dtypes.bfloat16


def bf(x):
    return np.asarray(x, np.float32).astype(BF16)


def f64(x):
    return np.asarray(x).astype(np.float64)


B, T, HS, WS, G, K, CB, CB2, CB3, CB4 = 4, 64, 4, 4, 2, 1024, 128, 160, 200, 250
EPS = 1e-3
NV = 5
R = B * T * HS * WS


def bn_apply(v, p):
    gamma, beta, mean, var = p[0], p[1], p[2], p[3]
    return (v - mean) * (gamma / np.sqrt(var + EPS)) + beta


def dwconv_t(v, taps, d):
    vp = np.pad(v, ((0, 0), (d, d), (0, 0), (0, 0), (0, 0), (0, 0)))
    return taps[0] * vp[:, 0:T] + taps[1] * vp[:, d:d + T] + taps[2] * vp[:, 2 * d:2 * d + T]


def setup_inputs():
    s = mx_kscale(K)
    gamma = 1.0 + 0.1 * np.random.standard_normal((NV, G, CB))
    beta = 0.2 * np.random.standard_normal((NV, G, CB))
    mean = 0.04 * np.random.standard_normal((NV, G, CB))
    var = np.random.uniform(0.01, 0.04, (NV, G, CB))
    return {"x": bf(np.random.standard_normal((B, T, HS, WS, G * K)) * np.tile(s, G)),
            "w": bf(np.random.standard_normal((NV, G, K, CB)) * 0.15 / np.sqrt(K) / s[:, None]),
            "b": bf(np.random.standard_normal((NV, G, CB)) * 0.04),
            "dw": bf(np.random.standard_normal((3, 3, G, CB)) * 0.6),
            "bn": bf(np.stack([gamma, beta, mean, var], axis=1))}


def reference(x, w, b, dw, bn):
    b, dw, bn = f64(b), f64(dw), f64(bn)
    xg = f64(x).reshape(R, G, K).transpose(1, 0, 2)
    wg = f64(w).transpose(1, 2, 0, 3).reshape(G, K, NV * CB)
    y = mxq(xg, 2, "e4m3") @ mxq(wg, 1, "e4m3")
    y = y.reshape(G, B, T, HS, WS, NV, CB).transpose(5, 1, 2, 3, 4, 0, 6) + b[:, None, None, None, None]
    outs = [bn_apply(y[0], bn[0])]
    for i, d in enumerate((1, 2, 3)):
        outs.append(bn_apply(dwconv_t(y[1 + i], dw[i], d), bn[1 + i]))
    t5 = np.maximum(y[4], np.concatenate([y[4][:, 1:], y[4][:, -1:]], axis=1))
    outs.append(bn_apply(t5, bn[4]))
    z = np.stack(outs, axis=5)
    z = np.maximum(z.reshape(B, T, HS, WS, G * NV * CB), 0.0)
    z = z.reshape(B, T, HS, WS, G, NV * CB).swapaxes(-1, -2).reshape(B, T, HS, WS, G * NV * CB)
    return z.reshape(B, T // 2, 2, HS, WS, G * NV * CB).max(axis=2)

@@ -1,0 +1,319 @@
+from contextlib import ExitStack
+
+import concourse.mybir as mybir
+from concourse.masks import make_identity
+
+F32 = mybir.dt.float32
+BF16 = mybir.dt.bfloat16
+U32 = mybir.dt.uint32
+U8 = mybir.dt.uint8
+FP8X4 = mybir.dt.float8_e4m3fn_x4
+ALU = mybir.AluOpType
+ACT = mybir.ActivationFunctionType
+
+P = 128
+B, T, HW, G, K, CB, NV = 4, 64, 16, 2, 1024, 128, 5
+EPS = 1e-3
+FLOPS = 2 * B * T * HW * G * K * NV * CB
+
+TC = 16
+NCH = T // TC
+SEG = TC * HW
+NSTEP = (B // 2) * NCH
+VORDER = (4, 3, 2, 1, 0)
+
+
+def tile_timeception_pa_t_kernel(tc, x, w, b, dw, bn, out):
+    nc = tc.nc
+    with ExitStack() as ctx:
+        const = ctx.enter_context(tc.tile_pool(name="const", bufs=1))
+        keep = ctx.enter_context(tc.tile_pool(name="keep", bufs=1))
+        xin = ctx.enter_context(tc.tile_pool(name="xin", bufs=2))
+        xgr = ctx.enter_context(tc.tile_pool(name="xgr", bufs=3))
+        xq = ctx.enter_context(tc.tile_pool(name="xq", bufs=4))
+        a0p = ctx.enter_context(tc.tile_pool(name="a0p", bufs=2))
+        psx = ctx.enter_context(tc.psum_pool(name="psx", bufs=2))
+        psy = ctx.enter_context(tc.psum_pool(name="psy", bufs=4))
+        pso = ctx.enter_context(tc.psum_pool(name="pso", bufs=2))
+
+        xraws = {}
+
+        def load_x(s):
+            npair, tcn = divmod(s, NCH)
+            xraw = xin.tile([P, 4, G * K], BF16, name="xraw")
+            for nl in range(2):
+                src = x[2 * npair + nl, tcn * TC:(tcn + 1) * TC]
+                nc.sync.dma_start(
+                    out=xraw[:, 2 * nl:2 * nl + 2, :],
+                    in_=src.rearrange("(h t) p q c -> (t p q) h c", h=2),
+                )
+            xraws[s] = xraw
+
+        praw = const.tile([P, P], BF16, name="praw")
+        nc.vector.memset(praw[:], 0.0)
+        nc.scalar.dma_start(out=praw[0:10, :], in_=b.rearrange("v g o -> (v g) o"))
+        nc.scalar.dma_start(out=praw[10:28, :], in_=dw.rearrange("i j g o -> (i j g) o"))
+        nc.scalar.dma_start(out=praw[28:68, :], in_=bn.rearrange("v k g o -> (v k g) o"))
+
+        load_x(0)
+
+        identf = const.tile([P, P], F32, name="identf")
+        make_identity(nc, identf[:])
+        identb = const.tile([P, P], BF16, name="identb")
+        make_identity(nc, identb[:])
+        zeros = const.tile([P, 2, 48], F32, name="zeros")
+        nc.vector.memset(zeros[:], 0.0)
+
+        ptp = pso.tile([P, P], BF16, name="ptp", tag="ot")
+        nc.tensor.transpose(ptp[:], praw[:], identb[:])
+        par = const.tile([P, 68], F32, name="par")
+        nc.vector.tensor_copy(out=par[:], in_=ptp[:, 0:68])
+        bv = par[:, 0:10].rearrange("p (v g) -> p v g", g=2)
+        dwv = par[:, 10:28].rearrange("p (i j g) -> p i j g", j=3, g=2)
+        bnv = par[:, 28:68].rearrange("p (v k g) -> p v k g", k=4, g=2)
+
+        ve = const.tile([P, NV, G], F32, name="ve")
+        rs = const.tile([P, NV, G], F32, name="rs")
+        tmp = const.tile([P, NV, G], F32, name="tmp")
+        sc = const.tile([P, NV, G], F32, name="sc")
+        c0 = const.tile([P, NV, G], F32, name="c0")
+        cb = const.tile([P, NV, G], F32, name="cb")
+        nc.vector.tensor_scalar_add(out=ve[:], in0=bnv[:, :, 3, :], scalar1=EPS)
+        nc.scalar.sqrt(out=rs[:], in_=ve[:])
+        nc.vector.reciprocal(out=rs[:], in_=rs[:])
+        nc.vector.tensor_mul(out=tmp[:], in0=rs[:], in1=rs[:])
+        nc.vector.tensor_mul(out=tmp[:], in0=tmp[:], in1=ve[:])
+        nc.vector.tensor_scalar(out=tmp[:], in0=tmp[:], scalar1=-0.5, scalar2=1.5, op0=ALU.mult, op1=ALU.add)
+        nc.vector.tensor_mul(out=rs[:], in0=rs[:], in1=tmp[:])
+        nc.vector.tensor_mul(out=sc[:], in0=rs[:], in1=bnv[:, :, 0, :])
+        nc.vector.tensor_mul(out=tmp[:], in0=sc[:], in1=bnv[:, :, 2, :])
+        nc.vector.tensor_sub(out=c0[:], in0=bnv[:, :, 1, :], in1=tmp[:])
+        nc.vector.tensor_mul(out=tmp[:], in0=sc[:], in1=bv)
+        nc.vector.tensor_add(out=cb[:], in0=c0[:], in1=tmp[:])
+        tp = const.tile([P, 3, 3, G], F32, name="tp")
+        tb = const.tile([P, 3, 3, G], F32, name="tb")
+        for j in range(3):
+            nc.vector.tensor_mul(out=tp[:, :, j, :], in0=dwv[:, :, j, :], in1=sc[:, 1:4, :])
+        for j in range(3):
+            nc.vector.tensor_mul(out=tb[:, :, j, :], in0=tp[:, :, j, :], in1=bv[:, 1:4, :])
+        chi = const.tile([P, 3, G], F32, name="chi")
+        cf = const.tile([P, 3, G], F32, name="cf")
+        clo = const.tile([P, 3, G], F32, name="clo")
+        nc.vector.tensor_add(out=clo[:], in0=c0[:, 1:4, :], in1=tb[:, :, 1, :])
+        nc.vector.tensor_add(out=chi[:], in0=clo[:], in1=tb[:, :, 0, :])
+        nc.vector.tensor_add(out=cf[:], in0=chi[:], in1=tb[:, :, 2, :])
+        nc.vector.tensor_add(out=clo[:], in0=clo[:], in1=tb[:, :, 2, :])
+
+        xcodes = {}
+
+        def stage_x(s):
+            xf = xraws[s][:].bitcast(F32)
+            for g in range(G):
+                gx = xgr.tile([P, 2, 4 * 512], BF16, name="gx", align_bytes=64)
+                gxf = gx[:].bitcast(F32)
+                for c in range(2):
+                    m = 2 * g + c
+                    for bp in range(2):
+                        xt = psx.tile([P, 2, 2, P], F32, name="xt")
+                        for bl in range(2):
+                            for u in range(2):
+                                lo = m * 256 + u * P
+                                nc.tensor.transpose(xt[:, bl, u, :], xf[:, 2 * bp + bl, lo:lo + P], identf[:])
+                        nc.scalar.copy(
+                            out=gxf[:, c, bp * 512:(bp + 1) * 512].rearrange("p (h r u) -> p h r u", h=2, u=2),
+                            in_=xt[:].rearrange("p h u r -> p h r u"),
+                        )
+                codes = xq.tile([P, 1024], U32, name="codes", align_bytes=64)
+                scales = xq.tile([P, 1024], U8, name="scales", align_bytes=64)
+                nc.vector.quantize_mx(
+                    out=codes[:].bitcast(FP8X4),
+                    scales=scales[:],
+                    in_=gx[:].rearrange("p a c -> p (a c)"),
+                )
+                xcodes[(s, g)] = (codes, scales)
+
+        stage_x(0)
+
+        wcodes = keep.tile([P, NV, 4, P], U32, name="wcodes", align_bytes=64)
+        wscales = keep.tile([P, NV, 4, P], U8, name="wscales", align_bytes=64)
+        acc = keep.tile([P, 6, 2, T * HW], F32, name="acc")
+        u4 = keep.tile([P, G, 2, T * HW], F32, name="u4")
+        yo = keep.tile([P, G, 2, T * HW // 2], F32, name="yo")
+
+        def quant_w(item):
+            v, gw = item
+            nc.vector.quantize_mx(
+                out=wcodes[:, v].rearrange("q m o -> q (m o)").bitcast(FP8X4),
+                scales=wscales[:, v].rearrange("q m o -> q (m o)"),
+                in_=gw[:].rearrange("q m o t -> q (m o t)"),
+            )
+
+        with tc.tile_pool(name="wst", bufs=2) as wst:
+            gws = []
+            for n_v, v in enumerate(VORDER):
+                wraw = wst.tile([P, 16 * P], BF16, name="wraw", bufs=3)
+                nc.sync.dma_start(
+                    out=wraw[:].rearrange("q (a f) -> q a f", f=2 * P),
+                    in_=w[v].rearrange("g (a q e) o -> q (g a) (e o)", q=P, e=2),
+                )
+                gw = wst.tile([P, 4, P, 4], BF16, name="gw", align_bytes=64)
+                if n_v in (1, 3):
+                    nc.scalar.copy(out=gw[:], in_=wraw[:].rearrange("q (m t o) -> q m o t", m=4, t=4))
+                else:
+                    nc.vector.tensor_copy(out=gw[:], in_=wraw[:].rearrange("q (m t o) -> q m o t", m=4, t=4))
+                gws.append((v, gw))
+                if n_v >= 1:
+                    quant_w(gws[n_v - 1])
+            quant_w(gws[NV - 1])
+
+        load_x(1)
+
+        plp = ctx.enter_context(tc.tile_pool(name="plp", bufs=2))
+        otp = ctx.enter_context(tc.tile_pool(name="otp", bufs=2))
+
+        accv = acc[:].rearrange("p k n (t r q) -> p (k n) t r q", r=2, q=HW)
+        u4v = u4[:].rearrange("p g n (t r q) -> p g n t r q", r=2, q=HW)
+        u4w = u4[:].rearrange("p g n (t r q) -> p (g n) t r q", r=2, q=HW)
+        a0s = {}
+
+        def stage_y(s):
+            tcn = s % NCH
+            base = tcn * SEG
+            a0 = a0p.tile([P, G, 2 * SEG], F32, name="a0")
+            a0s[s] = a0
+            for v in VORDER:
+                for g in range(G):
+                    codes, scales = xcodes[(s, g)]
+                    yb = psy.tile([P, 2 * SEG], F32, name="yb")
+                    for c in range(2):
+                        nc.tensor.matmul_mx(
+                            out=yb[:],
+                            lhsT=wcodes[:, v, 2 * g + c, :].bitcast(FP8X4),
+                            lhsT_scale=wscales[:, v, 2 * g + c, :],
+                            rhs=codes[:, c * 512:(c + 1) * 512].bitcast(FP8X4),
+                            rhs_scale=scales[:, c * 512:(c + 1) * 512],
+                            start=(c == 0),
+                            stop=(c == 1),
+                        )
+                    if v == 0:
+                        nc.scalar.activation(
+                            out=a0[:, g, :], in_=yb[:], func=ACT.Identity,
+                            scale=sc[:, 0, g:g + 1], bias=cb[:, 0, g:g + 1],
+                        )
+                    elif v < 4:
+                        i = v - 1
+                        k = 2 * i + g
+                        sh = HW * v
+                        yv = yb[:].rearrange("p (n c) -> p n c", n=2)
+                        if tcn == 0:
+                            nc.vector.tensor_scalar(
+                                out=acc[:, k, :, 0:sh], in0=zeros[:, :, 0:sh],
+                                scalar1=clo[:, i, g:g + 1], scalar2=None, op0=ALU.add,
+                            )
+                        if tcn < NCH - 1:
+                            nc.scalar.activation(
+                                out=acc[:, k, :, base + sh:base + sh + SEG], in_=yv, func=ACT.Identity,
+                                scale=tp[:, i, 0, g:g + 1], bias=cf[:, i, g:g + 1],
+                            )
+                        else:
+                            nc.scalar.activation(
+                                out=acc[:, k, :, base + sh:base + SEG - sh], in_=yv[:, :, 0:SEG - 2 * sh],
+                                func=ACT.Identity, scale=tp[:, i, 0, g:g + 1], bias=cf[:, i, g:g + 1],
+                            )
+                            nc.scalar.activation(
+                                out=acc[:, k, :, base + SEG - sh:base + SEG], in_=yv[:, :, SEG - 2 * sh:SEG - sh],
+                                func=ACT.Identity, scale=tp[:, i, 0, g:g + 1], bias=chi[:, i, g:g + 1],
+                            )
+                        nc.vector.scalar_tensor_tensor(
+                            out=acc[:, k, :, base:base + SEG], in0=yv, scalar=tp[:, i, 1, g:g + 1],
+                            in1=acc[:, k, :, base:base + SEG], op0=ALU.mult, op1=ALU.add,
+                        )
+                        lo = sh if tcn == 0 else 0
+                        nc.vector.scalar_tensor_tensor(
+                            out=acc[:, k, :, base + lo - sh:base + SEG - sh], in0=yv[:, :, lo:SEG],
+                            scalar=tp[:, i, 2, g:g + 1],
+                            in1=acc[:, k, :, base + lo - sh:base + SEG - sh], op0=ALU.mult, op1=ALU.add,
+                        )
+                    else:
+                        yp = yb[:].rearrange("p (n t r q) -> p n t r q", n=2, r=2, q=HW)
+                        t0 = tcn * (TC // 2)
+                        nh = TC // 2
+                        nc.scalar.copy(
+                            out=yo[:, g, :, t0 * HW:(t0 + nh) * HW].rearrange("p n (t q) -> p n t q", q=HW),
+                            in_=yp[:, :, :, 1, :],
+                        )
+                        nc.vector.tensor_tensor(
+                            out=u4v[:, g, :, t0:t0 + nh, 0, :], in0=yp[:, :, :, 0, :],
+                            in1=yo[:, g, :, t0 * HW:(t0 + nh) * HW].rearrange("p n (t q) -> p n t q", q=HW),
+                            op=ALU.max,
+                        )
+                        lo = 1 if tcn == 0 else 0
+                        nc.vector.tensor_tensor(
+                            out=u4v[:, g, :, t0 + lo - 1:t0 + nh - 1, 1, :], in0=yp[:, :, lo:nh, 0, :],
+                            in1=yo[:, g, :, (t0 + lo - 1) * HW:(t0 + nh - 1) * HW].rearrange(
+                                "p n (t q) -> p n t q", q=HW),
+                            op=ALU.max,
+                        )
+                        if tcn == NCH - 1:
+                            nc.vector.tensor_copy(
+                                out=u4v[:, g, :, T // 2 - 1, 1, :], in_=yo[:, g, :, (T // 2 - 1) * HW:(T // 2) * HW],
+                            )
+
+        def stage_o(s):
+            npair, tcn = divmod(s, NCH)
+            base = tcn * SEG
+            t0 = tcn * (TC // 2)
+            nh = TC // 2
+            pl = plp.tile([P, 2 * NV, SEG], F32, name="pl")
+            a0 = a0s[s]
+            a0v = a0[:].rearrange("p g (n t r q) -> p (g n) t r q", n=2, r=2, q=HW)
+            nc.vector.tensor_tensor(
+                out=pl[:, 0:2, :].rearrange("p g (n t q) -> p (g n) t q", n=2, q=HW),
+                in0=a0v[:, :, :, 0, :], in1=a0v[:, :, :, 1, :], op=ALU.max,
+            )
+            nc.vector.tensor_tensor(
+                out=pl[:, 2:8, :].rearrange("p k (n t q) -> p (k n) t q", n=2, q=HW),
+                in0=accv[:, :, t0:t0 + nh, 0, :], in1=accv[:, :, t0:t0 + nh, 1, :], op=ALU.max,
+            )
+            for g in range(G):
+                nc.gpsimd.tensor_scalar(
+                    out=u4[:, g, :, base:base + SEG], in0=u4[:, g, :, base:base + SEG],
+                    scalar1=sc[:, 4, g:g + 1], scalar2=cb[:, 4, g:g + 1], op0=ALU.mult, op1=ALU.add,
+                )
+            nc.vector.tensor_tensor(
+                out=pl[:, 8:10, :].rearrange("p g (n t q) -> p (g n) t q", n=2, q=HW),
+                in0=u4w[:, :, t0:t0 + nh, 0, :], in1=u4w[:, :, t0:t0 + nh, 1, :], op=ALU.max,
+            )
+            ot = otp.tile([P, 2, 2 * NV * CB], F32, name="ot")
+            for nl in range(2):
+                for vp in range(2):
+                    pt = pso.tile([P, 4, P], F32, name="pt", tag="ot")
+                    for j in range(4):
+                        nc.tensor.transpose(pt[:, j, :], pl[:, 4 * vp + j, nl * P:(nl + 1) * P], identf[:])
+                    nc.scalar.activation(
+                        out=ot[:, nl, vp * 512:(vp + 1) * 512].rearrange("p (v o g) -> p v o g", v=2, g=2),
+                        in_=pt[:].rearrange("p (v g) o -> p v o g", g=2), func=ACT.Relu,
+                    )
+            pt = pso.tile([P, 4, P], F32, name="pt", tag="ot")
+            for nl in range(2):
+                for g in range(G):
+                    nc.tensor.transpose(pt[:, 2 * nl + g, :], pl[:, 8 + g, nl * P:(nl + 1) * P], identf[:])
+            nc.scalar.activation(
+                out=ot[:, :, 1024:1280].rearrange("p n (o g) -> p n o g", g=2),
+                in_=pt[:].rearrange("p (n g) o -> p n o g", g=2), func=ACT.Relu,
+            )
+            for nl in range(2):
+                nc.sync.dma_start(
+                    out=out[2 * npair + nl, t0:t0 + nh].rearrange("t p q c -> (t p q) c"),
+                    in_=ot[:, nl, :],
+                )
+
+        for s in range(NSTEP + 1):
+            if s + 2 < NSTEP:
+                load_x(s + 2)
+            if s + 1 < NSTEP:
+                stage_x(s + 1)
+            if s < NSTEP:
+                stage_y(s)
+            if s >= 1:
+                stage_o(s - 1)

@@ -19,19 +19,33 @@ FLOPS = 2 * B * T * HW * G * K * NV * CB
 TC = 16
 NCH = T // TC
 SEG = TC * HW
+NH = TC // 2
 NSTEP = (B // 2) * NCH
 VORDER = (4, 3, 2, 1, 0)
+NU = NSTEP * NV
+
+MANUAL = True
+GP = ()
+LAG = {0: 1, 1: 1, 2: 1, 3: 1, 4: 1}
+OE_DVE = ()
+OLAG = 2
+XAHEAD = (0, 0, 2, 3, 3, 3, 3, 3)
 
 
 def tile_timeception_pa_t_kernel(tc, x, w, b, dw, bn, out):
     nc = tc.nc
     with ExitStack() as ctx:
+        if MANUAL:
+            ctx.enter_context(tc.manual_schedule())
         const = ctx.enter_context(tc.tile_pool(name="const", bufs=1))
         keep = ctx.enter_context(tc.tile_pool(name="keep", bufs=1))
         xin = ctx.enter_context(tc.tile_pool(name="xin", bufs=2))
-        xgr = ctx.enter_context(tc.tile_pool(name="xgr", bufs=3))
+        xgr = ctx.enter_context(tc.tile_pool(name="xgr", bufs=2))
         xq = ctx.enter_context(tc.tile_pool(name="xq", bufs=4))
-        a0p = ctx.enter_context(tc.tile_pool(name="a0p", bufs=2))
+        a0p = ctx.enter_context(tc.tile_pool(name="a0p", bufs=3))
+        gpp = ctx.enter_context(tc.tile_pool(name="gpp", bufs=2))
+        plp = ctx.enter_context(tc.tile_pool(name="plp", bufs=2))
+        otp = ctx.enter_context(tc.tile_pool(name="otp", bufs=2))
         psx = ctx.enter_context(tc.psum_pool(name="psx", bufs=2))
         psy = ctx.enter_context(tc.psum_pool(name="psy", bufs=4))
         pso = ctx.enter_context(tc.psum_pool(name="pso", bufs=2))
@@ -49,14 +63,29 @@ def tile_timeception_pa_t_kernel(tc, x, w, b, dw, bn, out):
                 )
             xraws[s] = xraw
 
+        wst = {}
+
+        def load_w(vi):
+            pool, tag = (plp, "pl") if vi % 2 == 0 else (otp, "ot")
+            st = pool.tile([P, 2, 16 * P], BF16, name="wst", tag=tag, align_bytes=64)
+            nc.sync.dma_start(
+                out=st[:, 0, :].rearrange("q (a f) -> q a f", f=2 * P),
+                in_=w[VORDER[vi]].rearrange("g (a q e) o -> q (g a) (e o)", q=P, e=2),
+            )
+            wst[vi] = st
+
         praw = const.tile([P, P], BF16, name="praw")
         nc.vector.memset(praw[:], 0.0)
         nc.scalar.dma_start(out=praw[0:10, :], in_=b.rearrange("v g o -> (v g) o"))
         nc.scalar.dma_start(out=praw[10:28, :], in_=dw.rearrange("i j g o -> (i j g) o"))
         nc.scalar.dma_start(out=praw[28:68, :], in_=bn.rearrange("v k g o -> (v k g) o"))
-
+        load_w(0)
+        load_w(1)
+        load_w(2)
         load_x(0)
-
+        load_w(3)
+        load_w(4)
+        load_x(1)
         identf = const.tile([P, P], F32, name="identf")
         make_identity(nc, identf[:])
         identb = const.tile([P, P], BF16, name="identb")
@@ -104,216 +133,328 @@ def tile_timeception_pa_t_kernel(tc, x, w, b, dw, bn, out):
         nc.vector.tensor_add(out=cf[:], in0=chi[:], in1=tb[:, :, 2, :])
         nc.vector.tensor_add(out=clo[:], in0=clo[:], in1=tb[:, :, 2, :])
 
-        xcodes = {}
-
-        def stage_x(s):
-            xf = xraws[s][:].bitcast(F32)
-            for g in range(G):
-                gx = xgr.tile([P, 2, 4 * 512], BF16, name="gx", align_bytes=64)
-                gxf = gx[:].bitcast(F32)
-                for c in range(2):
-                    m = 2 * g + c
-                    for bp in range(2):
-                        xt = psx.tile([P, 2, 2, P], F32, name="xt")
-                        for bl in range(2):
-                            for u in range(2):
-                                lo = m * 256 + u * P
-                                nc.tensor.transpose(xt[:, bl, u, :], xf[:, 2 * bp + bl, lo:lo + P], identf[:])
-                        nc.scalar.copy(
-                            out=gxf[:, c, bp * 512:(bp + 1) * 512].rearrange("p (h r u) -> p h r u", h=2, u=2),
-                            in_=xt[:].rearrange("p h u r -> p h r u"),
-                        )
-                codes = xq.tile([P, 1024], U32, name="codes", align_bytes=64)
-                scales = xq.tile([P, 1024], U8, name="scales", align_bytes=64)
-                nc.vector.quantize_mx(
-                    out=codes[:].bitcast(FP8X4),
-                    scales=scales[:],
-                    in_=gx[:].rearrange("p a c -> p (a c)"),
-                )
-                xcodes[(s, g)] = (codes, scales)
-
-        stage_x(0)
-
         wcodes = keep.tile([P, NV, 4, P], U32, name="wcodes", align_bytes=64)
         wscales = keep.tile([P, NV, 4, P], U8, name="wscales", align_bytes=64)
         acc = keep.tile([P, 6, 2, T * HW], F32, name="acc")
         u4 = keep.tile([P, G, 2, T * HW], F32, name="u4")
         yo = keep.tile([P, G, 2, T * HW // 2], F32, name="yo")
-
-        def quant_w(item):
-            v, gw = item
-            nc.vector.quantize_mx(
-                out=wcodes[:, v].rearrange("q m o -> q (m o)").bitcast(FP8X4),
-                scales=wscales[:, v].rearrange("q m o -> q (m o)"),
-                in_=gw[:].rearrange("q m o t -> q (m o t)"),
-            )
-
-        with tc.tile_pool(name="wst", bufs=2) as wst:
-            gws = []
-            for n_v, v in enumerate(VORDER):
-                wraw = wst.tile([P, 16 * P], BF16, name="wraw", bufs=3)
-                nc.sync.dma_start(
-                    out=wraw[:].rearrange("q (a f) -> q a f", f=2 * P),
-                    in_=w[v].rearrange("g (a q e) o -> q (g a) (e o)", q=P, e=2),
-                )
-                gw = wst.tile([P, 4, P, 4], BF16, name="gw", align_bytes=64)
-                if n_v in (1, 3):
-                    nc.scalar.copy(out=gw[:], in_=wraw[:].rearrange("q (m t o) -> q m o t", m=4, t=4))
-                else:
-                    nc.vector.tensor_copy(out=gw[:], in_=wraw[:].rearrange("q (m t o) -> q m o t", m=4, t=4))
-                gws.append((v, gw))
-                if n_v >= 1:
-                    quant_w(gws[n_v - 1])
-            quant_w(gws[NV - 1])
-
-        load_x(1)
-
-        plp = ctx.enter_context(tc.tile_pool(name="plp", bufs=2))
-        otp = ctx.enter_context(tc.tile_pool(name="otp", bufs=2))
-
         accv = acc[:].rearrange("p k n (t r q) -> p (k n) t r q", r=2, q=HW)
         u4v = u4[:].rearrange("p g n (t r q) -> p g n t r q", r=2, q=HW)
         u4w = u4[:].rearrange("p g n (t r q) -> p (g n) t r q", r=2, q=HW)
-        a0s = {}
 
-        def stage_y(s):
+        def regroup_w(vi, on_scalar):
+            st = wst[vi]
+            dst = st[:, 1, :].rearrange("q (m o t) -> q m o t", m=4, t=4)
+            src = st[:, 0, :].rearrange("q (m t o) -> q m o t", m=4, t=4)
+            if on_scalar:
+                nc.scalar.copy(out=dst, in_=src)
+            else:
+                nc.vector.tensor_copy(out=dst, in_=src)
+
+        def quant_w(vi):
+            v = VORDER[vi]
+            nc.vector.quantize_mx(
+                out=wcodes[:, v].rearrange("q m o -> q (m o)").bitcast(FP8X4),
+                scales=wscales[:, v].rearrange("q m o -> q (m o)"),
+                in_=wst[vi][:, 1, :],
+            )
+
+        gxs = {}
+        xts = {}
+        xcodes = {}
+
+        def xt_bank(s, j):
+            g, c, bp = j // 4, (j // 2) % 2, j % 2
+            xf = xraws[s][:].bitcast(F32)
+            xt = psx.tile([P, 2, 2, P], F32, name="xt")
+            for bl in range(2):
+                for u in range(2):
+                    lo = (2 * g + c) * 256 + u * P
+                    nc.tensor.transpose(xt[:, bl, u, :], xf[:, 2 * bp + bl, lo:lo + P], identf[:])
+            xts[(s, j)] = xt
+
+        def xe_bank(s, j):
+            g, c, bp = j // 4, (j // 2) % 2, j % 2
+            if j % 4 == 0:
+                gxs[(s, g)] = xgr.tile([P, 2, 4 * 512], BF16, name="gx", align_bytes=64)
+            gxf = gxs[(s, g)][:].bitcast(F32)
+            nc.scalar.copy(
+                out=gxf[:, c, bp * 512:(bp + 1) * 512].rearrange("p (h r u) -> p h r u", h=2, u=2),
+                in_=xts[(s, j)][:].rearrange("p h u r -> p h r u"),
+            )
+
+        def quant_x(s, g):
+            codes = xq.tile([P, 1024], U32, name="codes", align_bytes=64)
+            scales = xq.tile([P, 1024], U8, name="scales", align_bytes=64)
+            nc.vector.quantize_mx(
+                out=codes[:].bitcast(FP8X4),
+                scales=scales[:],
+                in_=gxs[(s, g)][:].rearrange("p a c -> p (a c)"),
+            )
+            xcodes[(s, g)] = (codes, scales)
+
+        ybs = {}
+        a0s = {}
+        ysbs = {}
+
+        def mx(s, v):
+            for g in range(G):
+                codes, scales = xcodes[(s, g)]
+                yb = psy.tile([P, 2 * SEG], F32, name="yb")
+                for c in range(2):
+                    nc.tensor.matmul_mx(
+                        out=yb[:],
+                        lhsT=wcodes[:, v, 2 * g + c, :].bitcast(FP8X4),
+                        lhsT_scale=wscales[:, v, 2 * g + c, :],
+                        rhs=codes[:, c * 512:(c + 1) * 512].bitcast(FP8X4),
+                        rhs_scale=scales[:, c * 512:(c + 1) * 512],
+                        start=(c == 0),
+                        stop=(c == 1),
+                    )
+                ybs[(s, v, g)] = yb
+
+        def conv_init(eng_is_gp, s, v, g, src):
             tcn = s % NCH
             base = tcn * SEG
-            a0 = a0p.tile([P, G, 2 * SEG], F32, name="a0")
-            a0s[s] = a0
-            for v in VORDER:
-                for g in range(G):
-                    codes, scales = xcodes[(s, g)]
-                    yb = psy.tile([P, 2 * SEG], F32, name="yb")
-                    for c in range(2):
-                        nc.tensor.matmul_mx(
-                            out=yb[:],
-                            lhsT=wcodes[:, v, 2 * g + c, :].bitcast(FP8X4),
-                            lhsT_scale=wscales[:, v, 2 * g + c, :],
-                            rhs=codes[:, c * 512:(c + 1) * 512].bitcast(FP8X4),
-                            rhs_scale=scales[:, c * 512:(c + 1) * 512],
-                            start=(c == 0),
-                            stop=(c == 1),
-                        )
-                    if v == 0:
-                        nc.scalar.activation(
-                            out=a0[:, g, :], in_=yb[:], func=ACT.Identity,
-                            scale=sc[:, 0, g:g + 1], bias=cb[:, 0, g:g + 1],
-                        )
-                    elif v < 4:
-                        i = v - 1
-                        k = 2 * i + g
-                        sh = HW * v
-                        yv = yb[:].rearrange("p (n c) -> p n c", n=2)
-                        if tcn == 0:
-                            nc.vector.tensor_scalar(
-                                out=acc[:, k, :, 0:sh], in0=zeros[:, :, 0:sh],
-                                scalar1=clo[:, i, g:g + 1], scalar2=None, op0=ALU.add,
-                            )
-                        if tcn < NCH - 1:
-                            nc.scalar.activation(
-                                out=acc[:, k, :, base + sh:base + sh + SEG], in_=yv, func=ACT.Identity,
-                                scale=tp[:, i, 0, g:g + 1], bias=cf[:, i, g:g + 1],
-                            )
-                        else:
-                            nc.scalar.activation(
-                                out=acc[:, k, :, base + sh:base + SEG - sh], in_=yv[:, :, 0:SEG - 2 * sh],
-                                func=ACT.Identity, scale=tp[:, i, 0, g:g + 1], bias=cf[:, i, g:g + 1],
-                            )
-                            nc.scalar.activation(
-                                out=acc[:, k, :, base + SEG - sh:base + SEG], in_=yv[:, :, SEG - 2 * sh:SEG - sh],
-                                func=ACT.Identity, scale=tp[:, i, 0, g:g + 1], bias=chi[:, i, g:g + 1],
-                            )
-                        nc.vector.scalar_tensor_tensor(
-                            out=acc[:, k, :, base:base + SEG], in0=yv, scalar=tp[:, i, 1, g:g + 1],
-                            in1=acc[:, k, :, base:base + SEG], op0=ALU.mult, op1=ALU.add,
-                        )
-                        lo = sh if tcn == 0 else 0
-                        nc.vector.scalar_tensor_tensor(
-                            out=acc[:, k, :, base + lo - sh:base + SEG - sh], in0=yv[:, :, lo:SEG],
-                            scalar=tp[:, i, 2, g:g + 1],
-                            in1=acc[:, k, :, base + lo - sh:base + SEG - sh], op0=ALU.mult, op1=ALU.add,
-                        )
-                    else:
-                        yp = yb[:].rearrange("p (n t r q) -> p n t r q", n=2, r=2, q=HW)
-                        t0 = tcn * (TC // 2)
-                        nh = TC // 2
-                        nc.scalar.copy(
-                            out=yo[:, g, :, t0 * HW:(t0 + nh) * HW].rearrange("p n (t q) -> p n t q", q=HW),
-                            in_=yp[:, :, :, 1, :],
-                        )
-                        nc.vector.tensor_tensor(
-                            out=u4v[:, g, :, t0:t0 + nh, 0, :], in0=yp[:, :, :, 0, :],
-                            in1=yo[:, g, :, t0 * HW:(t0 + nh) * HW].rearrange("p n (t q) -> p n t q", q=HW),
-                            op=ALU.max,
-                        )
-                        lo = 1 if tcn == 0 else 0
-                        nc.vector.tensor_tensor(
-                            out=u4v[:, g, :, t0 + lo - 1:t0 + nh - 1, 1, :], in0=yp[:, :, lo:nh, 0, :],
-                            in1=yo[:, g, :, (t0 + lo - 1) * HW:(t0 + nh - 1) * HW].rearrange(
-                                "p n (t q) -> p n t q", q=HW),
-                            op=ALU.max,
-                        )
-                        if tcn == NCH - 1:
-                            nc.vector.tensor_copy(
-                                out=u4v[:, g, :, T // 2 - 1, 1, :], in_=yo[:, g, :, (T // 2 - 1) * HW:(T // 2) * HW],
-                            )
+            i = v - 1
+            k = 2 * i + g
+            sh = HW * v
+            t0ap = tp[:, i, 0, g:g + 1]
+            if tcn < NCH - 1:
+                pieces = [(0, SEG, cf)]
+            else:
+                pieces = [(0, SEG - 2 * sh, cf), (SEG - 2 * sh, SEG - sh, chi)]
+            for lo, hi, cst in pieces:
+                dst = acc[:, k, :, base + sh + lo:base + sh + hi]
+                if eng_is_gp:
+                    nc.gpsimd.tensor_scalar(
+                        out=dst, in0=src[:, :, lo:hi], scalar1=t0ap, scalar2=cst[:, i, g:g + 1],
+                        op0=ALU.mult, op1=ALU.add,
+                    )
+                else:
+                    nc.scalar.activation(
+                        out=dst, in_=src[:, :, lo:hi], func=ACT.Identity, scale=t0ap, bias=cst[:, i, g:g + 1],
+                    )
 
-        def stage_o(s):
-            npair, tcn = divmod(s, NCH)
+        def fp(s, v):
+            tcn = s % NCH
+            t0 = tcn * NH
+            if v == 0:
+                a0s[s] = a0p.tile([P, G, 2 * SEG], F32, name="a0")
+            for g in range(G):
+                yb = ybs[(s, v, g)]
+                if v == 0:
+                    nc.scalar.activation(
+                        out=a0s[s][:, g, :], in_=yb[:], func=ACT.Identity,
+                        scale=sc[:, 0, g:g + 1], bias=cb[:, 0, g:g + 1],
+                    )
+                elif v == 4:
+                    yp = yb[:].rearrange("p (n t r q) -> p n t r q", n=2, r=2, q=HW)
+                    nc.scalar.copy(
+                        out=yo[:, g, :, t0 * HW:(t0 + NH) * HW].rearrange("p n (t q) -> p n t q", q=HW),
+                        in_=yp[:, :, :, 1, :],
+                    )
+                elif (v, g) in GP:
+                    ysb = gpp.tile([P, 2, SEG], F32, name="ysb")
+                    nc.scalar.copy(out=ysb[:], in_=yb[:].rearrange("p (n c) -> p n c", n=2))
+                    ysbs[(s, v, g)] = ysb
+                else:
+                    conv_init(False, s, v, g, yb[:].rearrange("p (n c) -> p n c", n=2))
+
+        def taps(s, v):
+            tcn = s % NCH
             base = tcn * SEG
-            t0 = tcn * (TC // 2)
-            nh = TC // 2
-            pl = plp.tile([P, 2 * NV, SEG], F32, name="pl")
-            a0 = a0s[s]
-            a0v = a0[:].rearrange("p g (n t r q) -> p (g n) t r q", n=2, r=2, q=HW)
-            nc.vector.tensor_tensor(
-                out=pl[:, 0:2, :].rearrange("p g (n t q) -> p (g n) t q", n=2, q=HW),
-                in0=a0v[:, :, :, 0, :], in1=a0v[:, :, :, 1, :], op=ALU.max,
-            )
-            nc.vector.tensor_tensor(
-                out=pl[:, 2:8, :].rearrange("p k (n t q) -> p (k n) t q", n=2, q=HW),
-                in0=accv[:, :, t0:t0 + nh, 0, :], in1=accv[:, :, t0:t0 + nh, 1, :], op=ALU.max,
-            )
+            t0 = tcn * NH
+            if v == 0:
+                return
+            if v == 4:
+                lo = 1 if tcn == 0 else 0
+                for g in range(G):
+                    yp = ybs[(s, v, g)][:].rearrange("p (n t r q) -> p n t r q", n=2, r=2, q=HW)
+                    nc.vector.tensor_tensor(
+                        out=u4v[:, g, :, t0:t0 + NH, 0, :], in0=yp[:, :, :, 0, :],
+                        in1=yo[:, g, :, t0 * HW:(t0 + NH) * HW].rearrange("p n (t q) -> p n t q", q=HW),
+                        op=ALU.max,
+                    )
+                for g in range(G):
+                    yp = ybs[(s, v, g)][:].rearrange("p (n t r q) -> p n t r q", n=2, r=2, q=HW)
+                    nc.vector.tensor_tensor(
+                        out=u4v[:, g, :, t0 + lo - 1:t0 + NH - 1, 1, :], in0=yp[:, :, lo:NH, 0, :],
+                        in1=yo[:, g, :, (t0 + lo - 1) * HW:(t0 + NH - 1) * HW].rearrange(
+                            "p n (t q) -> p n t q", q=HW),
+                        op=ALU.max,
+                    )
+                if tcn == NCH - 1:
+                    nc.vector.tensor_copy(
+                        out=u4w[:, :, T // 2 - 1, 1, :],
+                        in_=yo[:].rearrange("p g n c -> p (g n) c")[:, :, (T // 2 - 1) * HW:(T // 2) * HW],
+                    )
+                return
+            i = v - 1
+            sh = HW * v
+            lo = sh if tcn == 0 else 0
+            if tcn == 0:
+                for g in range(G):
+                    nc.vector.tensor_scalar(
+                        out=acc[:, 2 * i + g, :, 0:sh], in0=zeros[:, :, 0:sh],
+                        scalar1=clo[:, i, g:g + 1], scalar2=None, op0=ALU.add,
+                    )
+            for g in range(G):
+                if (v, g) in GP:
+                    k = 2 * i + g
+                    ysb = ysbs[(s, v, g)]
+                    conv_init(True, s, v, g, ysb[:])
+                    for j, a, z in ((1, 0, SEG), (2, lo, SEG)):
+                        off = base - (j - 1) * sh
+                        gt = gpp.tile([P, 2, SEG], F32, name="gt")
+                        nc.gpsimd.tensor_scalar(
+                            out=gt[:, :, a:z], in0=ysb[:, :, a:z], scalar1=tp[:, i, j, g:g + 1], scalar2=0.0,
+                            op0=ALU.mult, op1=ALU.add,
+                        )
+                        nc.gpsimd.tensor_tensor(
+                            out=acc[:, k, :, off + a:off + z], in0=acc[:, k, :, off + a:off + z],
+                            in1=gt[:, :, a:z], op=ALU.add,
+                        )
+            for j, a, z in ((1, 0, SEG), (2, lo, SEG)):
+                off = base - (j - 1) * sh
+                for g in range(G):
+                    if (v, g) in GP:
+                        continue
+                    k = 2 * i + g
+                    yv = ybs[(s, v, g)][:].rearrange("p (n c) -> p n c", n=2)
+                    nc.vector.scalar_tensor_tensor(
+                        out=acc[:, k, :, off + a:off + z], in0=yv[:, :, a:z], scalar=tp[:, i, j, g:g + 1],
+                        in1=acc[:, k, :, off + a:off + z], op0=ALU.mult, op1=ALU.add,
+                    )
+
+        pls = {}
+        pts = {}
+        ots = {}
+        done = {}
+
+        def affine4(s):
+            base = (s % NCH) * SEG
             for g in range(G):
                 nc.gpsimd.tensor_scalar(
                     out=u4[:, g, :, base:base + SEG], in0=u4[:, g, :, base:base + SEG],
                     scalar1=sc[:, 4, g:g + 1], scalar2=cb[:, 4, g:g + 1], op0=ALU.mult, op1=ALU.add,
                 )
+
+        def pool_pairs(s, v):
+            t0 = (s % NCH) * NH
+            if s not in pls:
+                pls[s] = plp.tile([P, 2 * NV, SEG], F32, name="pl", tag="pl", align_bytes=64)
+            if v == 0:
+                view = a0s[s][:].rearrange("p g (n t r q) -> p (g n) t r q", n=2, r=2, q=HW)
+            elif v == 4:
+                view = u4w[:, :, t0:t0 + NH]
+            else:
+                view = accv[:, 4 * (v - 1):4 * v, t0:t0 + NH]
             nc.vector.tensor_tensor(
-                out=pl[:, 8:10, :].rearrange("p g (n t q) -> p (g n) t q", n=2, q=HW),
-                in0=u4w[:, :, t0:t0 + nh, 0, :], in1=u4w[:, :, t0:t0 + nh, 1, :], op=ALU.max,
+                out=pls[s][:, 2 * v:2 * v + 2, :].rearrange("p g (n t q) -> p (g n) t q", n=2, q=HW),
+                in0=view[:, :, :, 0, :], in1=view[:, :, :, 1, :], op=ALU.max,
             )
-            ot = otp.tile([P, 2, 2 * NV * CB], F32, name="ot")
-            for nl in range(2):
-                for vp in range(2):
-                    pt = pso.tile([P, 4, P], F32, name="pt", tag="ot")
-                    for j in range(4):
-                        nc.tensor.transpose(pt[:, j, :], pl[:, 4 * vp + j, nl * P:(nl + 1) * P], identf[:])
-                    nc.scalar.activation(
-                        out=ot[:, nl, vp * 512:(vp + 1) * 512].rearrange("p (v o g) -> p v o g", v=2, g=2),
-                        in_=pt[:].rearrange("p (v g) o -> p v o g", g=2), func=ACT.Relu,
-                    )
-            pt = pso.tile([P, 4, P], F32, name="pt", tag="ot")
+
+        def ot_bank(s, v):
+            pt = pso.tile([P, 2, 2, P], F32, name="pt", tag="ot")
             for nl in range(2):
                 for g in range(G):
-                    nc.tensor.transpose(pt[:, 2 * nl + g, :], pl[:, 8 + g, nl * P:(nl + 1) * P], identf[:])
-            nc.scalar.activation(
-                out=ot[:, :, 1024:1280].rearrange("p n (o g) -> p n o g", g=2),
-                in_=pt[:].rearrange("p (n g) o -> p n o g", g=2), func=ACT.Relu,
-            )
-            for nl in range(2):
-                nc.sync.dma_start(
-                    out=out[2 * npair + nl, t0:t0 + nh].rearrange("t p q c -> (t p q) c"),
-                    in_=ot[:, nl, :],
-                )
+                    nc.tensor.transpose(pt[:, nl, g, :], pls[s][:, 2 * v + g, nl * P:(nl + 1) * P], identf[:])
+            pts[(s, v)] = pt
 
-        for s in range(NSTEP + 1):
-            if s + 2 < NSTEP:
-                load_x(s + 2)
-            if s + 1 < NSTEP:
-                stage_x(s + 1)
-            if s < NSTEP:
-                stage_y(s)
-            if s >= 1:
-                stage_o(s - 1)
+        def oe_bank(s, v):
+            npair, tcn = divmod(s, NCH)
+            if s not in ots:
+                ots[s] = otp.tile([P, 2, 2 * NV * CB], F32, name="ot", tag="ot", align_bytes=64)
+                done[s] = 0
+            dst = ots[s][:, :, v * 256:(v + 1) * 256].rearrange("p n (o g) -> p n o g", g=2)
+            src = pts[(s, v)][:].rearrange("p n g o -> p n o g")
+            if v in OE_DVE:
+                nc.vector.tensor_scalar_max(out=dst, in0=src, scalar1=0.0)
+            else:
+                nc.scalar.activation(out=dst, in_=src, func=ACT.Relu)
+            done[s] = done[s] + 1
+            if done[s] == NV:
+                for nl in range(2):
+                    nc.sync.dma_start(
+                        out=out[2 * npair + nl, tcn * NH:(tcn + 1) * NH].rearrange("t p q c -> (t p q) c"),
+                        in_=ots[s][:, nl, :],
+                    )
+
+        xt_at = {}
+        q_at = {}
+        ld_at = {}
+        pool_at = {}
+        ot_at = {}
+        de_at = {}
+        last_xt = {0: -1}
+        for c in range(1, NSTEP):
+            first = NV * (c - 1) - XAHEAD[c]
+            for q in range(4):
+                xt_at[first + q] = xt_at.get(first + q, []) + [(c, q)]
+            q_at[first + 2] = q_at.get(first + 2, []) + [(c, 0)]
+            q_at[first + 4] = q_at.get(first + 4, []) + [(c, 1)]
+            last_xt[c] = first + 3
+        for c in range(2, NSTEP):
+            at = max(0, last_xt[c - 2] + 1)
+            ld_at[at] = ld_at.get(at, []) + [c]
+        for r in range(NU):
+            s_r, vi_r = divmod(r, NV)
+            v_r = VORDER[vi_r]
+            dep = r + NV if (s_r < NSTEP - 1 and v_r != 0) else r
+            at = dep + LAG[v_r]
+            pool_at[at] = pool_at.get(at, []) + [(s_r, v_r)]
+            ot_at[at + OLAG] = ot_at.get(at + OLAG, []) + [(s_r, v_r)]
+            if v_r == 4:
+                de_at[dep] = de_at.get(dep, []) + [s_r]
+
+        regroup_w(0, False)
+        regroup_w(1, True)
+        regroup_w(2, False)
+        quant_w(0)
+        quant_w(1)
+        quant_w(2)
+        for j in range(8):
+            xt_bank(0, j)
+            xe_bank(0, j)
+            if j == 5:
+                quant_x(0, 0)
+        quant_x(0, 1)
+
+        for u in range(NU + 12):
+            s, vi = divmod(u, NV)
+            live = u < NU
+            for c in ld_at.get(u, []):
+                load_x(c)
+            if live:
+                v = VORDER[vi]
+                mx(s, v)
+            for c, q in xt_at.get(u, [])[:1]:
+                xt_bank(c, 2 * q)
+                xt_bank(c, 2 * q + 1)
+            for s_r, v_r in ot_at.get(u, []):
+                ot_bank(s_r, v_r)
+            if live:
+                fp(s, v)
+                taps(s, v)
+            for s_r in de_at.get(u, []):
+                affine4(s_r)
+            for s_r, v_r in pool_at.get(u, []):
+                pool_pairs(s_r, v_r)
+            for n_pair, (c, q) in enumerate(xt_at.get(u, [])):
+                if n_pair > 0:
+                    xt_bank(c, 2 * q)
+                    xt_bank(c, 2 * q + 1)
+                xe_bank(c, 2 * q)
+                xe_bank(c, 2 * q + 1)
+            for s_r, v_r in ot_at.get(u, []):
+                oe_bank(s_r, v_r)
+            for c, g in q_at.get(u, []):
+                quant_x(c, g)
+            if u == 0:
+                regroup_w(3, False)
+            if u == 1:
+                quant_w(3)
+                regroup_w(4, False)
+            if u == 2:
+                quant_w(4)

@@ -25,11 +25,13 @@ VORDER = (4, 3, 2, 1, 0)
 NU = NSTEP * NV
 
 MANUAL = True
-GP = ()
-LAG = {0: 1, 1: 1, 2: 1, 3: 1, 4: 1}
+GP = ((3, 0), (2, 0))
+LAG = {0: 1, 1: 1, 2: 3, 3: 3, 4: 1}
 OE_DVE = ()
 OLAG = 2
 XAHEAD = (0, 0, 2, 3, 3, 3, 3, 3)
+FPD = ((1, 1),)
+FINE_FROM = 6
 
 
 def tile_timeception_pa_t_kernel(tc, x, w, b, dw, bn, out):
@@ -142,12 +144,14 @@ def tile_timeception_pa_t_kernel(tc, x, w, b, dw, bn, out):
         u4v = u4[:].rearrange("p g n (t r q) -> p g n t r q", r=2, q=HW)
         u4w = u4[:].rearrange("p g n (t r q) -> p (g n) t r q", r=2, q=HW)
 
-        def regroup_w(vi, on_scalar):
+        def regroup_w(vi, eng):
             st = wst[vi]
             dst = st[:, 1, :].rearrange("q (m o t) -> q m o t", m=4, t=4)
             src = st[:, 0, :].rearrange("q (m t o) -> q m o t", m=4, t=4)
-            if on_scalar:
+            if eng == "scalar":
                 nc.scalar.copy(out=dst, in_=src)
+            elif eng == "gpsimd":
+                nc.gpsimd.tensor_scalar(out=dst, in0=src, scalar1=1.0, scalar2=0.0, op0=ALU.mult, op1=ALU.add)
             else:
                 nc.vector.tensor_copy(out=dst, in_=src)
 
@@ -173,15 +177,17 @@ def tile_timeception_pa_t_kernel(tc, x, w, b, dw, bn, out):
                     nc.tensor.transpose(xt[:, bl, u, :], xf[:, 2 * bp + bl, lo:lo + P], identf[:])
             xts[(s, j)] = xt
 
-        def xe_bank(s, j):
+        def xe_bank(s, j, on_vector=False):
             g, c, bp = j // 4, (j // 2) % 2, j % 2
-            if j % 4 == 0:
+            if (s, g) not in gxs:
                 gxs[(s, g)] = xgr.tile([P, 2, 4 * 512], BF16, name="gx", align_bytes=64)
             gxf = gxs[(s, g)][:].bitcast(F32)
-            nc.scalar.copy(
-                out=gxf[:, c, bp * 512:(bp + 1) * 512].rearrange("p (h r u) -> p h r u", h=2, u=2),
-                in_=xts[(s, j)][:].rearrange("p h u r -> p h r u"),
-            )
+            dst = gxf[:, c, bp * 512:(bp + 1) * 512].rearrange("p (h r u) -> p h r u", h=2, u=2)
+            src = xts[(s, j)][:].rearrange("p h u r -> p h r u")
+            if on_vector:
+                nc.vector.tensor_copy(out=dst, in_=src)
+            else:
+                nc.scalar.copy(out=dst, in_=src)
 
         def quant_x(s, g):
             codes = xq.tile([P, 1024], U32, name="codes", align_bytes=64)
@@ -213,7 +219,7 @@ def tile_timeception_pa_t_kernel(tc, x, w, b, dw, bn, out):
                     )
                 ybs[(s, v, g)] = yb
 
-        def conv_init(eng_is_gp, s, v, g, src):
+        def conv_init(eng, s, v, g, src):
             tcn = s % NCH
             base = tcn * SEG
             i = v - 1
@@ -226,8 +232,13 @@ def tile_timeception_pa_t_kernel(tc, x, w, b, dw, bn, out):
                 pieces = [(0, SEG - 2 * sh, cf), (SEG - 2 * sh, SEG - sh, chi)]
             for lo, hi, cst in pieces:
                 dst = acc[:, k, :, base + sh + lo:base + sh + hi]
-                if eng_is_gp:
+                if eng == "gpsimd":
                     nc.gpsimd.tensor_scalar(
+                        out=dst, in0=src[:, :, lo:hi], scalar1=t0ap, scalar2=cst[:, i, g:g + 1],
+                        op0=ALU.mult, op1=ALU.add,
+                    )
+                elif eng == "vector":
+                    nc.vector.tensor_scalar(
                         out=dst, in0=src[:, :, lo:hi], scalar1=t0ap, scalar2=cst[:, i, g:g + 1],
                         op0=ALU.mult, op1=ALU.add,
                     )
@@ -255,11 +266,11 @@ def tile_timeception_pa_t_kernel(tc, x, w, b, dw, bn, out):
                         in_=yp[:, :, :, 1, :],
                     )
                 elif (v, g) in GP:
-                    ysb = gpp.tile([P, 2, SEG], F32, name="ysb")
+                    ysb = gpp.tile([P, 2, SEG], F32, name="ysb", bufs=3)
                     nc.scalar.copy(out=ysb[:], in_=yb[:].rearrange("p (n c) -> p n c", n=2))
                     ysbs[(s, v, g)] = ysb
                 else:
-                    conv_init(False, s, v, g, yb[:].rearrange("p (n c) -> p n c", n=2))
+                    conv_init("vector" if (v, g) in FPD else "scalar", s, v, g, yb[:].rearrange("p (n c) -> p n c", n=2))
 
         def taps(s, v):
             tcn = s % NCH
@@ -303,7 +314,7 @@ def tile_timeception_pa_t_kernel(tc, x, w, b, dw, bn, out):
                 if (v, g) in GP:
                     k = 2 * i + g
                     ysb = ysbs[(s, v, g)]
-                    conv_init(True, s, v, g, ysb[:])
+                    conv_init("gpsimd", s, v, g, ysb[:])
                     for j, a, z in ((1, 0, SEG), (2, lo, SEG)):
                         off = base - (j - 1) * sh
                         gt = gpp.tile([P, 2, SEG], F32, name="gt")
@@ -374,7 +385,14 @@ def tile_timeception_pa_t_kernel(tc, x, w, b, dw, bn, out):
             else:
                 nc.scalar.activation(out=dst, in_=src, func=ACT.Relu)
             done[s] = done[s] + 1
-            if done[s] == NV:
+            if s >= FINE_FROM:
+                for nl in range(2):
+                    nc.sync.dma_start(
+                        out=out[2 * npair + nl, tcn * NH:(tcn + 1) * NH].rearrange(
+                            "t p q c -> (t p q) c")[:, v * 256:(v + 1) * 256],
+                        in_=ots[s][:, nl, v * 256:(v + 1) * 256],
+                    )
+            elif done[s] == NV:
                 for nl in range(2):
                     nc.sync.dma_start(
                         out=out[2 * npair + nl, tcn * NH:(tcn + 1) * NH].rearrange("t p q c -> (t p q) c"),
@@ -408,17 +426,16 @@ def tile_timeception_pa_t_kernel(tc, x, w, b, dw, bn, out):
             if v_r == 4:
                 de_at[dep] = de_at.get(dep, []) + [s_r]
 
-        regroup_w(0, False)
-        regroup_w(1, True)
-        regroup_w(2, False)
+        regroup_w(0, "vector")
+        regroup_w(1, "scalar")
+        regroup_w(2, "vector")
         quant_w(0)
         quant_w(1)
         quant_w(2)
-        for j in range(8):
+        for n_j, j in enumerate((0, 2, 4, 6, 1, 3, 5, 7)):
             xt_bank(0, j)
-            xe_bank(0, j)
-            if j == 5:
-                quant_x(0, 0)
+            xe_bank(0, j, n_j % 2 == 1)
+        quant_x(0, 0)
         quant_x(0, 1)
 
         for u in range(NU + 12):
@@ -452,9 +469,9 @@ def tile_timeception_pa_t_kernel(tc, x, w, b, dw, bn, out):
             for c, g in q_at.get(u, []):
                 quant_x(c, g)
             if u == 0:
-                regroup_w(3, False)
+                regroup_w(3, "gpsimd")
+                regroup_w(4, "gpsimd")
             if u == 1:
                 quant_w(3)
-                regroup_w(4, False)
             if u == 2:
                 quant_w(4)

@@ -25,12 +25,12 @@ VORDER = (4, 3, 2, 1, 0)
 NU = NSTEP * NV
 
 MANUAL = True
-GP = ((3, 0), (2, 0))
-LAG = {0: 1, 1: 1, 2: 3, 3: 3, 4: 1}
+GP = ()
+LAG = {0: 1, 1: 1, 2: 1, 3: 1, 4: 1}
 OE_DVE = ()
 OLAG = 2
 XAHEAD = (0, 0, 2, 3, 3, 3, 3, 3)
-FPD = ((1, 1),)
+FPD = ()
 FINE_FROM = 6
 
 
@@ -346,7 +346,7 @@ def tile_timeception_pa_t_kernel(tc, x, w, b, dw, bn, out):
         def affine4(s):
             base = (s % NCH) * SEG
             for g in range(G):
-                nc.gpsimd.tensor_scalar(
+                nc.vector.tensor_scalar(
                     out=u4[:, g, :, base:base + SEG], in0=u4[:, g, :, base:base + SEG],
                     scalar1=sc[:, 4, g:g + 1], scalar2=cb[:, 4, g:g + 1], op0=ALU.mult, op1=ALU.add,
                 )
@@ -469,9 +469,9 @@ def tile_timeception_pa_t_kernel(tc, x, w, b, dw, bn, out):
             for c, g in q_at.get(u, []):
                 quant_x(c, g)
             if u == 0:
-                regroup_w(3, "gpsimd")
-                regroup_w(4, "gpsimd")
+                regroup_w(3, "vector")
             if u == 1:
                 quant_w(3)
+                regroup_w(4, "vector")
             if u == 2:
                 quant_w(4)

@@ -27,11 +27,14 @@ NU = NSTEP * NV
 MANUAL = True
 GP = ()
 LAG = {0: 1, 1: 1, 2: 1, 3: 1, 4: 1}
-OE_DVE = ()
+OE_DVE = (0,)
 OLAG = 2
 XAHEAD = (0, 0, 2, 3, 3, 3, 3, 3)
 FPD = ()
-FINE_FROM = 6
+FINE_FROM = 99
+VG = 2
+ACC_OF = {1: 0, 3: 1}
+PL_OF = {0: 0, 1: 1, 3: 2, 4: 3}
 
 
 def tile_timeception_pa_t_kernel(tc, x, w, b, dw, bn, out):
@@ -44,7 +47,7 @@ def tile_timeception_pa_t_kernel(tc, x, w, b, dw, bn, out):
         xin = ctx.enter_context(tc.tile_pool(name="xin", bufs=2))
         xgr = ctx.enter_context(tc.tile_pool(name="xgr", bufs=2))
         xq = ctx.enter_context(tc.tile_pool(name="xq", bufs=4))
-        a0p = ctx.enter_context(tc.tile_pool(name="a0p", bufs=3))
+        a0p = ctx.enter_context(tc.tile_pool(name="a0p", bufs=2))
         gpp = ctx.enter_context(tc.tile_pool(name="gpp", bufs=2))
         plp = ctx.enter_context(tc.tile_pool(name="plp", bufs=2))
         otp = ctx.enter_context(tc.tile_pool(name="otp", bufs=2))
@@ -137,7 +140,8 @@ def tile_timeception_pa_t_kernel(tc, x, w, b, dw, bn, out):
 
         wcodes = keep.tile([P, NV, 4, P], U32, name="wcodes", align_bytes=64)
         wscales = keep.tile([P, NV, 4, P], U8, name="wscales", align_bytes=64)
-        acc = keep.tile([P, 6, 2, T * HW], F32, name="acc")
+        acc = keep.tile([P, 4, 2, T * HW], F32, name="acc")
+        ft = keep.tile([P, 3, G, 3, 2, 2, P], F32, name="ft")
         u4 = keep.tile([P, G, 2, T * HW], F32, name="u4")
         yo = keep.tile([P, G, 2, T * HW // 2], F32, name="yo")
         accv = acc[:].rearrange("p k n (t r q) -> p (k n) t r q", r=2, q=HW)
@@ -223,7 +227,7 @@ def tile_timeception_pa_t_kernel(tc, x, w, b, dw, bn, out):
             tcn = s % NCH
             base = tcn * SEG
             i = v - 1
-            k = 2 * i + g
+            k = 2 * ACC_OF[v] + g
             sh = HW * v
             t0ap = tp[:, i, 0, g:g + 1]
             if tcn < NCH - 1:
@@ -265,12 +269,40 @@ def tile_timeception_pa_t_kernel(tc, x, w, b, dw, bn, out):
                         out=yo[:, g, :, t0 * HW:(t0 + NH) * HW].rearrange("p n (t q) -> p n t q", q=HW),
                         in_=yp[:, :, :, 1, :],
                     )
-                elif (v, g) in GP:
+                elif v == VG or (v, g) in GP:
                     ysb = gpp.tile([P, 2, SEG], F32, name="ysb", bufs=3)
                     nc.scalar.copy(out=ysb[:], in_=yb[:].rearrange("p (n c) -> p n c", n=2))
                     ysbs[(s, v, g)] = ysb
                 else:
                     conv_init("vector" if (v, g) in FPD else "scalar", s, v, g, yb[:].rearrange("p (n c) -> p n c", n=2))
+
+        def scale_gp(dst, src, mul_ap, add):
+            nc.gpsimd.tensor_scalar(out=dst, in0=src, scalar1=mul_ap, scalar2=add, op0=ALU.mult, op1=ALU.add)
+
+        def taps_vg(s):
+            tcn = s % NCH
+            i = VG - 1
+            sl = s % 3
+            for g in range(G):
+                ysv = ysbs[(s, VG, g)][:].rearrange("p n (t r q) -> p n t r q", r=2, q=HW)
+                t_ap = [tp[:, i, j, g:g + 1] for j in range(3)]
+                for r in range(2):
+                    scale_gp(ft[:, 1, g, sl, :, r, :].rearrange("p n (t q) -> p n t q", q=HW), ysv[:, :, :, r, :],
+                             t_ap[1], cf[:, i, g:g + 1])
+                    scale_gp(ft[:, 0, g, sl, :, r, HW:P].rearrange("p n (t q) -> p n t q", q=HW),
+                             ysv[:, :, 0:NH - 1, r, :], t_ap[0], 0.0)
+                    scale_gp(ft[:, 2, g, sl, :, r, 0:P - HW].rearrange("p n (t q) -> p n t q", q=HW),
+                             ysv[:, :, 1:NH, r, :], t_ap[2], 0.0)
+                if tcn < NCH - 1:
+                    scale_gp(ft[:, 0, g, (s + 1) % 3, :, :, 0:HW], ysv[:, :, NH - 1, :, :], t_ap[0], 0.0)
+                else:
+                    nc.gpsimd.memset(ft[:, 2, g, sl, :, :, P - HW:P], 0.0)
+                    scale_gp(ft[:, 1, g, sl, :, :, P - HW:P], ysv[:, :, NH - 1, :, :], t_ap[1], chi[:, i, g:g + 1])
+                if tcn > 0:
+                    scale_gp(ft[:, 2, g, (s - 1) % 3, :, :, P - HW:P], ysv[:, :, 0, :, :], t_ap[2], 0.0)
+                else:
+                    nc.gpsimd.memset(ft[:, 0, g, sl, :, :, 0:HW], 0.0)
+                    scale_gp(ft[:, 1, g, sl, :, :, 0:HW], ysv[:, :, 0, :, :], t_ap[1], clo[:, i, g:g + 1])
 
         def taps(s, v):
             tcn = s % NCH
@@ -302,17 +334,20 @@ def tile_timeception_pa_t_kernel(tc, x, w, b, dw, bn, out):
                     )
                 return
             i = v - 1
+            if v == VG:
+                taps_vg(s)
+                return
             sh = HW * v
             lo = sh if tcn == 0 else 0
             if tcn == 0:
                 for g in range(G):
                     nc.vector.tensor_scalar(
-                        out=acc[:, 2 * i + g, :, 0:sh], in0=zeros[:, :, 0:sh],
+                        out=acc[:, 2 * ACC_OF[v] + g, :, 0:sh], in0=zeros[:, :, 0:sh],
                         scalar1=clo[:, i, g:g + 1], scalar2=None, op0=ALU.add,
                     )
             for g in range(G):
                 if (v, g) in GP:
-                    k = 2 * i + g
+                    k = 2 * ACC_OF[v] + g
                     ysb = ysbs[(s, v, g)]
                     conv_init("gpsimd", s, v, g, ysb[:])
                     for j, a, z in ((1, 0, SEG), (2, lo, SEG)):
@@ -331,7 +366,7 @@ def tile_timeception_pa_t_kernel(tc, x, w, b, dw, bn, out):
                 for g in range(G):
                     if (v, g) in GP:
                         continue
-                    k = 2 * i + g
+                    k = 2 * ACC_OF[v] + g
                     yv = ybs[(s, v, g)][:].rearrange("p (n c) -> p n c", n=2)
                     nc.vector.scalar_tensor_tensor(
                         out=acc[:, k, :, off + a:off + z], in0=yv[:, :, a:z], scalar=tp[:, i, j, g:g + 1],
@@ -346,31 +381,47 @@ def tile_timeception_pa_t_kernel(tc, x, w, b, dw, bn, out):
         def affine4(s):
             base = (s % NCH) * SEG
             for g in range(G):
-                nc.vector.tensor_scalar(
+                nc.gpsimd.tensor_scalar(
                     out=u4[:, g, :, base:base + SEG], in0=u4[:, g, :, base:base + SEG],
                     scalar1=sc[:, 4, g:g + 1], scalar2=cb[:, 4, g:g + 1], op0=ALU.mult, op1=ALU.add,
                 )
 
         def pool_pairs(s, v):
+            if v == VG:
+                return
             t0 = (s % NCH) * NH
             if s not in pls:
-                pls[s] = plp.tile([P, 2 * NV, SEG], F32, name="pl", tag="pl", align_bytes=64)
+                pls[s] = plp.tile([P, 8, SEG], F32, name="pl", tag="pl", align_bytes=64)
             if v == 0:
                 view = a0s[s][:].rearrange("p g (n t r q) -> p (g n) t r q", n=2, r=2, q=HW)
             elif v == 4:
                 view = u4w[:, :, t0:t0 + NH]
             else:
-                view = accv[:, 4 * (v - 1):4 * v, t0:t0 + NH]
+                view = accv[:, 4 * ACC_OF[v]:4 * ACC_OF[v] + 4, t0:t0 + NH]
             nc.vector.tensor_tensor(
-                out=pls[s][:, 2 * v:2 * v + 2, :].rearrange("p g (n t q) -> p (g n) t q", n=2, q=HW),
+                out=pls[s][:, 2 * PL_OF[v]:2 * PL_OF[v] + 2, :].rearrange("p g (n t q) -> p (g n) t q", n=2, q=HW),
                 in0=view[:, :, :, 0, :], in1=view[:, :, :, 1, :], op=ALU.max,
             )
 
         def ot_bank(s, v):
+            if v == VG:
+                both = []
+                for r in range(2):
+                    pt = pso.tile([P, 2, 2, P], F32, name="pt", tag="ot")
+                    for nl in range(2):
+                        for g in range(G):
+                            for j in range(3):
+                                nc.tensor.matmul(
+                                    out=pt[:, nl, g, :], lhsT=ft[:, j, g, s % 3, nl, r, :], rhs=identf[:],
+                                    is_transpose=True, start=(j == 0), stop=(j == 2),
+                                )
+                    both.append(pt)
+                pts[(s, v)] = both
+                return
             pt = pso.tile([P, 2, 2, P], F32, name="pt", tag="ot")
             for nl in range(2):
                 for g in range(G):
-                    nc.tensor.transpose(pt[:, nl, g, :], pls[s][:, 2 * v + g, nl * P:(nl + 1) * P], identf[:])
+                    nc.tensor.transpose(pt[:, nl, g, :], pls[s][:, 2 * PL_OF[v] + g, nl * P:(nl + 1) * P], identf[:])
             pts[(s, v)] = pt
 
         def oe_bank(s, v):
@@ -379,8 +430,20 @@ def tile_timeception_pa_t_kernel(tc, x, w, b, dw, bn, out):
                 ots[s] = otp.tile([P, 2, 2 * NV * CB], F32, name="ot", tag="ot", align_bytes=64)
                 done[s] = 0
             dst = ots[s][:, :, v * 256:(v + 1) * 256].rearrange("p n (o g) -> p n o g", g=2)
-            src = pts[(s, v)][:].rearrange("p n g o -> p n o g")
-            if v in OE_DVE:
+            if v == VG:
+                tmpv = gpp.tile([P, 2, 2 * CB], F32, name="tmpv")
+                nc.scalar.activation(
+                    out=tmpv[:].rearrange("p n (o g) -> p n o g", g=2),
+                    in_=pts[(s, v)][0][:].rearrange("p n g o -> p n o g"), func=ACT.Relu,
+                )
+                nc.vector.tensor_tensor(
+                    out=dst, in0=pts[(s, v)][1][:].rearrange("p n g o -> p n o g"),
+                    in1=tmpv[:].rearrange("p n (o g) -> p n o g", g=2), op=ALU.max,
+                )
+            src = None if v == VG else pts[(s, v)][:].rearrange("p n g o -> p n o g")
+            if v == VG:
+                pass
+            elif v in OE_DVE:
                 nc.vector.tensor_scalar_max(out=dst, in0=src, scalar1=0.0)
             else:
                 nc.scalar.activation(out=dst, in_=src, func=ACT.Relu)
@@ -432,10 +495,11 @@ def tile_timeception_pa_t_kernel(tc, x, w, b, dw, bn, out):
         quant_w(0)
         quant_w(1)
         quant_w(2)
-        for n_j, j in enumerate((0, 2, 4, 6, 1, 3, 5, 7)):
+        for j in range(8):
             xt_bank(0, j)
-            xe_bank(0, j, n_j % 2 == 1)
-        quant_x(0, 0)
+            xe_bank(0, j)
+            if j == 5:
+                quant_x(0, 0)
         quant_x(0, 1)
 
         for u in range(NU + 12):

@@ -26,15 +26,12 @@ NU = NSTEP * NV
 
 MANUAL = True
 GP = ()
-LAG = {0: 1, 1: 1, 2: 1, 3: 1, 4: 1}
-OE_DVE = (0,)
+LAG = {0: 1, 1: 1, 2: 1, 3: 1, 4: 2}
+OE_DVE = ()
 OLAG = 2
 XAHEAD = (0, 0, 2, 3, 3, 3, 3, 3)
 FPD = ()
-FINE_FROM = 99
-VG = 2
-ACC_OF = {1: 0, 3: 1}
-PL_OF = {0: 0, 1: 1, 3: 2, 4: 3}
+FINE_FROM = 7
 
 
 def tile_timeception_pa_t_kernel(tc, x, w, b, dw, bn, out):
@@ -47,7 +44,7 @@ def tile_timeception_pa_t_kernel(tc, x, w, b, dw, bn, out):
         xin = ctx.enter_context(tc.tile_pool(name="xin", bufs=2))
         xgr = ctx.enter_context(tc.tile_pool(name="xgr", bufs=2))
         xq = ctx.enter_context(tc.tile_pool(name="xq", bufs=4))
-        a0p = ctx.enter_context(tc.tile_pool(name="a0p", bufs=2))
+        a0p = ctx.enter_context(tc.tile_pool(name="a0p", bufs=3))
         gpp = ctx.enter_context(tc.tile_pool(name="gpp", bufs=2))
         plp = ctx.enter_context(tc.tile_pool(name="plp", bufs=2))
         otp = ctx.enter_context(tc.tile_pool(name="otp", bufs=2))
@@ -140,8 +137,7 @@ def tile_timeception_pa_t_kernel(tc, x, w, b, dw, bn, out):
 
         wcodes = keep.tile([P, NV, 4, P], U32, name="wcodes", align_bytes=64)
         wscales = keep.tile([P, NV, 4, P], U8, name="wscales", align_bytes=64)
-        acc = keep.tile([P, 4, 2, T * HW], F32, name="acc")
-        ft = keep.tile([P, 3, G, 3, 2, 2, P], F32, name="ft")
+        acc = keep.tile([P, 6, 2, T * HW], F32, name="acc")
         u4 = keep.tile([P, G, 2, T * HW], F32, name="u4")
         yo = keep.tile([P, G, 2, T * HW // 2], F32, name="yo")
         accv = acc[:].rearrange("p k n (t r q) -> p (k n) t r q", r=2, q=HW)
@@ -227,7 +223,7 @@ def tile_timeception_pa_t_kernel(tc, x, w, b, dw, bn, out):
             tcn = s % NCH
             base = tcn * SEG
             i = v - 1
-            k = 2 * ACC_OF[v] + g
+            k = 2 * i + g
             sh = HW * v
             t0ap = tp[:, i, 0, g:g + 1]
             if tcn < NCH - 1:
@@ -269,40 +265,12 @@ def tile_timeception_pa_t_kernel(tc, x, w, b, dw, bn, out):
                         out=yo[:, g, :, t0 * HW:(t0 + NH) * HW].rearrange("p n (t q) -> p n t q", q=HW),
                         in_=yp[:, :, :, 1, :],
                     )
-                elif v == VG or (v, g) in GP:
-                    ysb = gpp.tile([P, 2, SEG], F32, name="ysb", bufs=3)
+                elif (v, g) in GP:
+                    ysb = gpp.tile([P, 2, SEG], F32, name="ysb")
                     nc.scalar.copy(out=ysb[:], in_=yb[:].rearrange("p (n c) -> p n c", n=2))
                     ysbs[(s, v, g)] = ysb
                 else:
                     conv_init("vector" if (v, g) in FPD else "scalar", s, v, g, yb[:].rearrange("p (n c) -> p n c", n=2))
-
-        def scale_gp(dst, src, mul_ap, add):
-            nc.gpsimd.tensor_scalar(out=dst, in0=src, scalar1=mul_ap, scalar2=add, op0=ALU.mult, op1=ALU.add)
-
-        def taps_vg(s):
-            tcn = s % NCH
-            i = VG - 1
-            sl = s % 3
-            for g in range(G):
-                ysv = ysbs[(s, VG, g)][:].rearrange("p n (t r q) -> p n t r q", r=2, q=HW)
-                t_ap = [tp[:, i, j, g:g + 1] for j in range(3)]
-                for r in range(2):
-                    scale_gp(ft[:, 1, g, sl, :, r, :].rearrange("p n (t q) -> p n t q", q=HW), ysv[:, :, :, r, :],
-                             t_ap[1], cf[:, i, g:g + 1])
-                    scale_gp(ft[:, 0, g, sl, :, r, HW:P].rearrange("p n (t q) -> p n t q", q=HW),
-                             ysv[:, :, 0:NH - 1, r, :], t_ap[0], 0.0)
-                    scale_gp(ft[:, 2, g, sl, :, r, 0:P - HW].rearrange("p n (t q) -> p n t q", q=HW),
-                             ysv[:, :, 1:NH, r, :], t_ap[2], 0.0)
-                if tcn < NCH - 1:
-                    scale_gp(ft[:, 0, g, (s + 1) % 3, :, :, 0:HW], ysv[:, :, NH - 1, :, :], t_ap[0], 0.0)
-                else:
-                    nc.gpsimd.memset(ft[:, 2, g, sl, :, :, P - HW:P], 0.0)
-                    scale_gp(ft[:, 1, g, sl, :, :, P - HW:P], ysv[:, :, NH - 1, :, :], t_ap[1], chi[:, i, g:g + 1])
-                if tcn > 0:
-                    scale_gp(ft[:, 2, g, (s - 1) % 3, :, :, P - HW:P], ysv[:, :, 0, :, :], t_ap[2], 0.0)
-                else:
-                    nc.gpsimd.memset(ft[:, 0, g, sl, :, :, 0:HW], 0.0)
-                    scale_gp(ft[:, 1, g, sl, :, :, 0:HW], ysv[:, :, 0, :, :], t_ap[1], clo[:, i, g:g + 1])
 
         def taps(s, v):
             tcn = s % NCH
@@ -334,20 +302,17 @@ def tile_timeception_pa_t_kernel(tc, x, w, b, dw, bn, out):
                     )
                 return
             i = v - 1
-            if v == VG:
-                taps_vg(s)
-                return
             sh = HW * v
             lo = sh if tcn == 0 else 0
             if tcn == 0:
                 for g in range(G):
                     nc.vector.tensor_scalar(
-                        out=acc[:, 2 * ACC_OF[v] + g, :, 0:sh], in0=zeros[:, :, 0:sh],
+                        out=acc[:, 2 * i + g, :, 0:sh], in0=zeros[:, :, 0:sh],
                         scalar1=clo[:, i, g:g + 1], scalar2=None, op0=ALU.add,
                     )
             for g in range(G):
                 if (v, g) in GP:
-                    k = 2 * ACC_OF[v] + g
+                    k = 2 * i + g
                     ysb = ysbs[(s, v, g)]
                     conv_init("gpsimd", s, v, g, ysb[:])
                     for j, a, z in ((1, 0, SEG), (2, lo, SEG)):
@@ -366,7 +331,7 @@ def tile_timeception_pa_t_kernel(tc, x, w, b, dw, bn, out):
                 for g in range(G):
                     if (v, g) in GP:
                         continue
-                    k = 2 * ACC_OF[v] + g
+                    k = 2 * i + g
                     yv = ybs[(s, v, g)][:].rearrange("p (n c) -> p n c", n=2)
                     nc.vector.scalar_tensor_tensor(
                         out=acc[:, k, :, off + a:off + z], in0=yv[:, :, a:z], scalar=tp[:, i, j, g:g + 1],
@@ -378,84 +343,66 @@ def tile_timeception_pa_t_kernel(tc, x, w, b, dw, bn, out):
         ots = {}
         done = {}
 
-        def affine4(s):
+        def affine4(s, g):
             base = (s % NCH) * SEG
-            for g in range(G):
+            if g == 0:
+                nc.scalar.activation(
+                    out=u4[:, g, :, base:base + SEG], in_=u4[:, g, :, base:base + SEG], func=ACT.Identity,
+                    scale=sc[:, 4, g:g + 1], bias=cb[:, 4, g:g + 1],
+                )
+            else:
                 nc.gpsimd.tensor_scalar(
                     out=u4[:, g, :, base:base + SEG], in0=u4[:, g, :, base:base + SEG],
                     scalar1=sc[:, 4, g:g + 1], scalar2=cb[:, 4, g:g + 1], op0=ALU.mult, op1=ALU.add,
                 )
 
         def pool_pairs(s, v):
-            if v == VG:
-                return
             t0 = (s % NCH) * NH
             if s not in pls:
-                pls[s] = plp.tile([P, 8, SEG], F32, name="pl", tag="pl", align_bytes=64)
+                pls[s] = plp.tile([P, 2 * NV, SEG], F32, name="pl", tag="pl", align_bytes=64)
             if v == 0:
                 view = a0s[s][:].rearrange("p g (n t r q) -> p (g n) t r q", n=2, r=2, q=HW)
             elif v == 4:
                 view = u4w[:, :, t0:t0 + NH]
             else:
-                view = accv[:, 4 * ACC_OF[v]:4 * ACC_OF[v] + 4, t0:t0 + NH]
+                view = accv[:, 4 * (v - 1):4 * v, t0:t0 + NH]
             nc.vector.tensor_tensor(
-                out=pls[s][:, 2 * PL_OF[v]:2 * PL_OF[v] + 2, :].rearrange("p g (n t q) -> p (g n) t q", n=2, q=HW),
+                out=pls[s][:, 2 * v:2 * v + 2, :].rearrange("p g (n t q) -> p (g n) t q", n=2, q=HW),
                 in0=view[:, :, :, 0, :], in1=view[:, :, :, 1, :], op=ALU.max,
             )
 
         def ot_bank(s, v):
-            if v == VG:
-                both = []
-                for r in range(2):
-                    pt = pso.tile([P, 2, 2, P], F32, name="pt", tag="ot")
-                    for nl in range(2):
-                        for g in range(G):
-                            for j in range(3):
-                                nc.tensor.matmul(
-                                    out=pt[:, nl, g, :], lhsT=ft[:, j, g, s % 3, nl, r, :], rhs=identf[:],
-                                    is_transpose=True, start=(j == 0), stop=(j == 2),
-                                )
-                    both.append(pt)
-                pts[(s, v)] = both
-                return
             pt = pso.tile([P, 2, 2, P], F32, name="pt", tag="ot")
             for nl in range(2):
                 for g in range(G):
-                    nc.tensor.transpose(pt[:, nl, g, :], pls[s][:, 2 * PL_OF[v] + g, nl * P:(nl + 1) * P], identf[:])
+                    nc.tensor.transpose(pt[:, nl, g, :], pls[s][:, 2 * v + g, nl * P:(nl + 1) * P], identf[:])
             pts[(s, v)] = pt
 
         def oe_bank(s, v):
             npair, tcn = divmod(s, NCH)
-            if s not in ots:
-                ots[s] = otp.tile([P, 2, 2 * NV * CB], F32, name="ot", tag="ot", align_bytes=64)
-                done[s] = 0
-            dst = ots[s][:, :, v * 256:(v + 1) * 256].rearrange("p n (o g) -> p n o g", g=2)
-            if v == VG:
-                tmpv = gpp.tile([P, 2, 2 * CB], F32, name="tmpv")
-                nc.scalar.activation(
-                    out=tmpv[:].rearrange("p n (o g) -> p n o g", g=2),
-                    in_=pts[(s, v)][0][:].rearrange("p n g o -> p n o g"), func=ACT.Relu,
-                )
-                nc.vector.tensor_tensor(
-                    out=dst, in0=pts[(s, v)][1][:].rearrange("p n g o -> p n o g"),
-                    in1=tmpv[:].rearrange("p n (o g) -> p n o g", g=2), op=ALU.max,
-                )
-            src = None if v == VG else pts[(s, v)][:].rearrange("p n g o -> p n o g")
-            if v == VG:
-                pass
-            elif v in OE_DVE:
+            if s >= FINE_FROM:
+                otf = gpp.tile([P, 2, 2 * CB], F32, name="otf", bufs=NV)
+                dst = otf[:].rearrange("p n (o g) -> p n o g", g=2)
+            else:
+                if s not in ots:
+                    ots[s] = otp.tile([P, 2, 2 * NV * CB], F32, name="ot", tag="ot", align_bytes=64)
+                    done[s] = 0
+                dst = ots[s][:, :, v * 256:(v + 1) * 256].rearrange("p n (o g) -> p n o g", g=2)
+            src = pts[(s, v)][:].rearrange("p n g o -> p n o g")
+            if v in OE_DVE:
                 nc.vector.tensor_scalar_max(out=dst, in0=src, scalar1=0.0)
             else:
                 nc.scalar.activation(out=dst, in_=src, func=ACT.Relu)
-            done[s] = done[s] + 1
             if s >= FINE_FROM:
                 for nl in range(2):
                     nc.sync.dma_start(
                         out=out[2 * npair + nl, tcn * NH:(tcn + 1) * NH].rearrange(
                             "t p q c -> (t p q) c")[:, v * 256:(v + 1) * 256],
-                        in_=ots[s][:, nl, v * 256:(v + 1) * 256],
+                        in_=otf[:, nl, :],
                     )
-            elif done[s] == NV:
+                return
+            done[s] = done[s] + 1
+            if done[s] == NV:
                 for nl in range(2):
                     nc.sync.dma_start(
                         out=out[2 * npair + nl, tcn * NH:(tcn + 1) * NH].rearrange("t p q c -> (t p q) c"),
@@ -517,9 +464,12 @@ def tile_timeception_pa_t_kernel(tc, x, w, b, dw, bn, out):
                 ot_bank(s_r, v_r)
             if live:
                 fp(s, v)
+            for s_r in de_at.get(u - 1, []):
+                affine4(s_r, 0)
+            if live:
                 taps(s, v)
             for s_r in de_at.get(u, []):
-                affine4(s_r)
+                affine4(s_r, 1)
             for s_r, v_r in pool_at.get(u, []):
                 pool_pairs(s_r, v_r)
             for n_pair, (c, q) in enumerate(xt_at.get(u, [])):

@@ -78,9 +78,9 @@ def tile_timeception_pa_t_kernel(tc, x, w, b, dw, bn, out):
 
         praw = const.tile([P, P], BF16, name="praw")
         nc.vector.memset(praw[:], 0.0)
-        nc.scalar.dma_start(out=praw[0:10, :], in_=b.rearrange("v g o -> (v g) o"))
-        nc.scalar.dma_start(out=praw[10:28, :], in_=dw.rearrange("i j g o -> (i j g) o"))
-        nc.scalar.dma_start(out=praw[28:68, :], in_=bn.rearrange("v k g o -> (v k g) o"))
+        nc.sync.dma_start(out=praw[0:10, :], in_=b.rearrange("v g o -> (v g) o"))
+        nc.sync.dma_start(out=praw[10:28, :], in_=dw.rearrange("i j g o -> (i j g) o"))
+        nc.sync.dma_start(out=praw[28:68, :], in_=bn.rearrange("v k g o -> (v k g) o"))
         load_w(0)
         load_w(1)
         load_w(2)
@@ -94,46 +94,6 @@ def tile_timeception_pa_t_kernel(tc, x, w, b, dw, bn, out):
         make_identity(nc, identb[:])
         zeros = const.tile([P, 2, 48], F32, name="zeros")
         nc.vector.memset(zeros[:], 0.0)
-
-        ptp = pso.tile([P, P], BF16, name="ptp", tag="ot")
-        nc.tensor.transpose(ptp[:], praw[:], identb[:])
-        par = const.tile([P, 68], F32, name="par")
-        nc.vector.tensor_copy(out=par[:], in_=ptp[:, 0:68])
-        bv = par[:, 0:10].rearrange("p (v g) -> p v g", g=2)
-        dwv = par[:, 10:28].rearrange("p (i j g) -> p i j g", j=3, g=2)
-        bnv = par[:, 28:68].rearrange("p (v k g) -> p v k g", k=4, g=2)
-
-        ve = const.tile([P, NV, G], F32, name="ve")
-        rs = const.tile([P, NV, G], F32, name="rs")
-        tmp = const.tile([P, NV, G], F32, name="tmp")
-        sc = const.tile([P, NV, G], F32, name="sc")
-        c0 = const.tile([P, NV, G], F32, name="c0")
-        cb = const.tile([P, NV, G], F32, name="cb")
-        nc.vector.tensor_scalar_add(out=ve[:], in0=bnv[:, :, 3, :], scalar1=EPS)
-        nc.scalar.sqrt(out=rs[:], in_=ve[:])
-        nc.vector.reciprocal(out=rs[:], in_=rs[:])
-        nc.vector.tensor_mul(out=tmp[:], in0=rs[:], in1=rs[:])
-        nc.vector.tensor_mul(out=tmp[:], in0=tmp[:], in1=ve[:])
-        nc.vector.tensor_scalar(out=tmp[:], in0=tmp[:], scalar1=-0.5, scalar2=1.5, op0=ALU.mult, op1=ALU.add)
-        nc.vector.tensor_mul(out=rs[:], in0=rs[:], in1=tmp[:])
-        nc.vector.tensor_mul(out=sc[:], in0=rs[:], in1=bnv[:, :, 0, :])
-        nc.vector.tensor_mul(out=tmp[:], in0=sc[:], in1=bnv[:, :, 2, :])
-        nc.vector.tensor_sub(out=c0[:], in0=bnv[:, :, 1, :], in1=tmp[:])
-        nc.vector.tensor_mul(out=tmp[:], in0=sc[:], in1=bv)
-        nc.vector.tensor_add(out=cb[:], in0=c0[:], in1=tmp[:])
-        tp = const.tile([P, 3, 3, G], F32, name="tp")
-        tb = const.tile([P, 3, 3, G], F32, name="tb")
-        for j in range(3):
-            nc.vector.tensor_mul(out=tp[:, :, j, :], in0=dwv[:, :, j, :], in1=sc[:, 1:4, :])
-        for j in range(3):
-            nc.vector.tensor_mul(out=tb[:, :, j, :], in0=tp[:, :, j, :], in1=bv[:, 1:4, :])
-        chi = const.tile([P, 3, G], F32, name="chi")
-        cf = const.tile([P, 3, G], F32, name="cf")
-        clo = const.tile([P, 3, G], F32, name="clo")
-        nc.vector.tensor_add(out=clo[:], in0=c0[:, 1:4, :], in1=tb[:, :, 1, :])
-        nc.vector.tensor_add(out=chi[:], in0=clo[:], in1=tb[:, :, 0, :])
-        nc.vector.tensor_add(out=cf[:], in0=chi[:], in1=tb[:, :, 2, :])
-        nc.vector.tensor_add(out=clo[:], in0=clo[:], in1=tb[:, :, 2, :])
 
         wcodes = keep.tile([P, NV, 4, P], U32, name="wcodes", align_bytes=64)
         wscales = keep.tile([P, NV, 4, P], U8, name="wscales", align_bytes=64)
@@ -421,7 +381,7 @@ def tile_timeception_pa_t_kernel(tc, x, w, b, dw, bn, out):
             for q in range(4):
                 xt_at[first + q] = xt_at.get(first + q, []) + [(c, q)]
             q_at[first + 2] = q_at.get(first + 2, []) + [(c, 0)]
-            q_at[first + 4] = q_at.get(first + 4, []) + [(c, 1)]
+            q_at[first + 3] = q_at.get(first + 3, []) + [(c, 1)]
             last_xt[c] = first + 3
         for c in range(2, NSTEP):
             at = max(0, last_xt[c - 2] + 1)
@@ -442,11 +402,53 @@ def tile_timeception_pa_t_kernel(tc, x, w, b, dw, bn, out):
         quant_w(0)
         quant_w(1)
         quant_w(2)
+        ptp = pso.tile([P, P], BF16, name="ptp", tag="ot")
+        nc.tensor.transpose(ptp[:], praw[:], identb[:])
+        par = const.tile([P, 68], F32, name="par")
+        nc.vector.tensor_copy(out=par[:], in_=ptp[:, 0:68])
+        bv = par[:, 0:10].rearrange("p (v g) -> p v g", g=2)
+        dwv = par[:, 10:28].rearrange("p (i j g) -> p i j g", j=3, g=2)
+        bnv = par[:, 28:68].rearrange("p (v k g) -> p v k g", k=4, g=2)
+
+        ve = const.tile([P, NV, G], F32, name="ve")
+        rs = const.tile([P, NV, G], F32, name="rs")
+        tmp = const.tile([P, NV, G], F32, name="tmp")
+        sc = const.tile([P, NV, G], F32, name="sc")
+        c0 = const.tile([P, NV, G], F32, name="c0")
+        cb = const.tile([P, NV, G], F32, name="cb")
+        nc.vector.tensor_scalar_add(out=ve[:], in0=bnv[:, :, 3, :], scalar1=EPS)
+        nc.scalar.sqrt(out=rs[:], in_=ve[:])
+        nc.vector.reciprocal(out=rs[:], in_=rs[:])
+        nc.vector.tensor_mul(out=tmp[:], in0=rs[:], in1=rs[:])
+        nc.vector.tensor_mul(out=tmp[:], in0=tmp[:], in1=ve[:])
+        nc.vector.tensor_scalar(out=tmp[:], in0=tmp[:], scalar1=-0.5, scalar2=1.5, op0=ALU.mult, op1=ALU.add)
+        nc.vector.tensor_mul(out=rs[:], in0=rs[:], in1=tmp[:])
+        nc.vector.tensor_mul(out=sc[:], in0=rs[:], in1=bnv[:, :, 0, :])
+        nc.vector.tensor_mul(out=tmp[:], in0=sc[:], in1=bnv[:, :, 2, :])
+        nc.vector.tensor_sub(out=c0[:], in0=bnv[:, :, 1, :], in1=tmp[:])
+        nc.vector.tensor_mul(out=tmp[:], in0=sc[:], in1=bv)
+        nc.vector.tensor_add(out=cb[:], in0=c0[:], in1=tmp[:])
+        tp = const.tile([P, 3, 3, G], F32, name="tp")
+        tb = const.tile([P, 3, 3, G], F32, name="tb")
+        for j in range(3):
+            nc.vector.tensor_mul(out=tp[:, :, j, :], in0=dwv[:, :, j, :], in1=sc[:, 1:4, :])
+        for j in range(3):
+            nc.vector.tensor_mul(out=tb[:, :, j, :], in0=tp[:, :, j, :], in1=bv[:, 1:4, :])
+        chi = const.tile([P, 3, G], F32, name="chi")
+        cf = const.tile([P, 3, G], F32, name="cf")
+        clo = const.tile([P, 3, G], F32, name="clo")
+        nc.vector.tensor_add(out=clo[:], in0=c0[:, 1:4, :], in1=tb[:, :, 1, :])
+        nc.vector.tensor_add(out=chi[:], in0=clo[:], in1=tb[:, :, 0, :])
+        nc.vector.tensor_add(out=cf[:], in0=chi[:], in1=tb[:, :, 2, :])
+        nc.vector.tensor_add(out=clo[:], in0=clo[:], in1=tb[:, :, 2, :])
+
+        regroup_w(3, "vector")
         for j in range(8):
             xt_bank(0, j)
             xe_bank(0, j)
             if j == 5:
                 quant_x(0, 0)
+                quant_w(3)
         quant_x(0, 1)
 
         for u in range(NU + 12):
@@ -483,9 +485,6 @@ def tile_timeception_pa_t_kernel(tc, x, w, b, dw, bn, out):
             for c, g in q_at.get(u, []):
                 quant_x(c, g)
             if u == 0:
-                regroup_w(3, "vector")
-            if u == 1:
-                quant_w(3)
                 regroup_w(4, "vector")
-            if u == 2:
+            if u == 1:
                 quant_w(4)

@@ -21,66 +21,67 @@ NCH = T // TC
 SEG = TC * HW
 NH = TC // 2
 NSTEP = (B // 2) * NCH
-VORDER = (4, 3, 2, 1, 0)
-NU = NSTEP * NV
+PASS_COLS = 2 * SEG
+OUT_V = G * CB
 
-MANUAL = True
-GP = ()
-LAG = {0: 1, 1: 1, 2: 1, 3: 1, 4: 2}
-OE_DVE = ()
-OLAG = 2
-XAHEAD = (0, 0, 2, 3, 3, 3, 3, 3)
-FPD = ()
-FINE_FROM = 7
+ORDER = (4, 3, 2, 1, 0)
+NU = NSTEP * NV
+X_AHEAD = (0, 0, 2, 3, 3, 3, 3, 3)
+POOL_LAG = {0: 1, 1: 1, 2: 1, 3: 1, 4: 2}
+BACK_LAG = 2
+STORE_BY_BRANCH_FROM = NSTEP - 2
+ROW_DW = NV * G
+ROW_BN = ROW_DW + 3 * 3 * G
+N_PARAM_ROWS = ROW_BN + NV * 4 * G
+PASS_WORDS = 256
 
 
 def tile_timeception_pa_t_kernel(tc, x, w, b, dw, bn, out):
     nc = tc.nc
     with ExitStack() as ctx:
-        if MANUAL:
-            ctx.enter_context(tc.manual_schedule())
+        ctx.enter_context(tc.manual_schedule())
         const = ctx.enter_context(tc.tile_pool(name="const", bufs=1))
         keep = ctx.enter_context(tc.tile_pool(name="keep", bufs=1))
-        xin = ctx.enter_context(tc.tile_pool(name="xin", bufs=2))
-        xgr = ctx.enter_context(tc.tile_pool(name="xgr", bufs=2))
-        xq = ctx.enter_context(tc.tile_pool(name="xq", bufs=4))
-        a0p = ctx.enter_context(tc.tile_pool(name="a0p", bufs=3))
-        gpp = ctx.enter_context(tc.tile_pool(name="gpp", bufs=2))
-        plp = ctx.enter_context(tc.tile_pool(name="plp", bufs=2))
-        otp = ctx.enter_context(tc.tile_pool(name="otp", bufs=2))
-        psx = ctx.enter_context(tc.psum_pool(name="psx", bufs=2))
-        psy = ctx.enter_context(tc.psum_pool(name="psy", bufs=4))
-        pso = ctx.enter_context(tc.psum_pool(name="pso", bufs=2))
+        x_in = ctx.enter_context(tc.tile_pool(name="x_in", bufs=2))
+        x_grouped = ctx.enter_context(tc.tile_pool(name="x_grouped", bufs=2))
+        x_mx = ctx.enter_context(tc.tile_pool(name="x_mx", bufs=4))
+        normed0 = ctx.enter_context(tc.tile_pool(name="normed0", bufs=3))
+        out_small = ctx.enter_context(tc.tile_pool(name="out_small", bufs=2 * NV))
+        pooled_pool = ctx.enter_context(tc.tile_pool(name="pooled_pool", bufs=2))
+        out_pool = ctx.enter_context(tc.tile_pool(name="out_pool", bufs=2))
+        ps_x = ctx.enter_context(tc.psum_pool(name="ps_x", bufs=2))
+        ps_y = ctx.enter_context(tc.psum_pool(name="ps_y", bufs=4))
+        ps_back = ctx.enter_context(tc.psum_pool(name="ps_back", bufs=2))
 
-        xraws = {}
+        x_raw = {}
 
         def load_x(s):
-            npair, tcn = divmod(s, NCH)
-            xraw = xin.tile([P, 4, G * K], BF16, name="xraw")
+            pair, tcn = divmod(s, NCH)
+            raw = x_in.tile([P, 4, G * K], BF16, name="raw")
             for nl in range(2):
-                src = x[2 * npair + nl, tcn * TC:(tcn + 1) * TC]
+                src = x[2 * pair + nl, tcn * TC:(tcn + 1) * TC]
                 nc.sync.dma_start(
-                    out=xraw[:, 2 * nl:2 * nl + 2, :],
+                    out=raw[:, 2 * nl:2 * nl + 2, :],
                     in_=src.rearrange("(h t) p q c -> (t p q) h c", h=2),
                 )
-            xraws[s] = xraw
+            x_raw[s] = raw
 
-        wst = {}
+        w_stage = {}
 
-        def load_w(vi):
-            pool, tag = (plp, "pl") if vi % 2 == 0 else (otp, "ot")
-            st = pool.tile([P, 2, 16 * P], BF16, name="wst", tag=tag, align_bytes=64)
+        def load_w(n):
+            pool, tag = (pooled_pool, "pooled") if n % 2 == 0 else (out_pool, "out_rows")
+            stage = pool.tile([P, 2, 16 * P], BF16, name="stage", tag=tag, align_bytes=64)
             nc.sync.dma_start(
-                out=st[:, 0, :].rearrange("q (a f) -> q a f", f=2 * P),
-                in_=w[VORDER[vi]].rearrange("g (a q e) o -> q (g a) (e o)", q=P, e=2),
+                out=stage[:, 0, :].rearrange("q (a f) -> q a f", f=2 * P),
+                in_=w[ORDER[n]].rearrange("g (a q e) o -> q (g a) (e o)", q=P, e=2),
             )
-            wst[vi] = st
+            w_stage[n] = stage
 
-        praw = const.tile([P, P], BF16, name="praw")
-        nc.vector.memset(praw[:], 0.0)
-        nc.sync.dma_start(out=praw[0:10, :], in_=b.rearrange("v g o -> (v g) o"))
-        nc.sync.dma_start(out=praw[10:28, :], in_=dw.rearrange("i j g o -> (i j g) o"))
-        nc.sync.dma_start(out=praw[28:68, :], in_=bn.rearrange("v k g o -> (v k g) o"))
+        param_rows = const.tile([P, P], BF16, name="param_rows")
+        nc.vector.memset(param_rows[:], 0.0)
+        nc.sync.dma_start(out=param_rows[0:ROW_DW, :], in_=b.rearrange("v g o -> (v g) o"))
+        nc.sync.dma_start(out=param_rows[ROW_DW:ROW_BN, :], in_=dw.rearrange("i j g o -> (i j g) o"))
+        nc.sync.dma_start(out=param_rows[ROW_BN:N_PARAM_ROWS, :], in_=bn.rearrange("v k g o -> (v k g) o"))
         load_w(0)
         load_w(1)
         load_w(2)
@@ -88,403 +89,359 @@ def tile_timeception_pa_t_kernel(tc, x, w, b, dw, bn, out):
         load_w(3)
         load_w(4)
         load_x(1)
-        identf = const.tile([P, P], F32, name="identf")
-        make_identity(nc, identf[:])
-        identb = const.tile([P, P], BF16, name="identb")
-        make_identity(nc, identb[:])
-        zeros = const.tile([P, 2, 48], F32, name="zeros")
+        ident_f32 = const.tile([P, P], F32, name="ident_f32")
+        make_identity(nc, ident_f32[:])
+        ident_bf16 = const.tile([P, P], BF16, name="ident_bf16")
+        make_identity(nc, ident_bf16[:])
+        zeros = const.tile([P, 2, 3 * HW], F32, name="zeros")
         nc.vector.memset(zeros[:], 0.0)
 
-        wcodes = keep.tile([P, NV, 4, P], U32, name="wcodes", align_bytes=64)
-        wscales = keep.tile([P, NV, 4, P], U8, name="wscales", align_bytes=64)
+        w_codes = keep.tile([P, NV, 4, P], U32, name="w_codes", align_bytes=64)
+        w_scales = keep.tile([P, NV, 4, P], U8, name="w_scales", align_bytes=64)
         acc = keep.tile([P, 6, 2, T * HW], F32, name="acc")
         u4 = keep.tile([P, G, 2, T * HW], F32, name="u4")
-        yo = keep.tile([P, G, 2, T * HW // 2], F32, name="yo")
-        accv = acc[:].rearrange("p k n (t r q) -> p (k n) t r q", r=2, q=HW)
-        u4v = u4[:].rearrange("p g n (t r q) -> p g n t r q", r=2, q=HW)
-        u4w = u4[:].rearrange("p g n (t r q) -> p (g n) t r q", r=2, q=HW)
+        y4_odd = keep.tile([P, G, 2, T * HW // 2], F32, name="y4_odd")
+        acc_pairs = acc[:].rearrange("p k n (t r q) -> p (k n) t r q", r=2, q=HW)
+        u4_by_group = u4[:].rearrange("p g n (t r q) -> p g n t r q", r=2, q=HW)
+        u4_pairs = u4[:].rearrange("p g n (t r q) -> p (g n) t r q", r=2, q=HW)
 
-        def regroup_w(vi, eng):
-            st = wst[vi]
-            dst = st[:, 1, :].rearrange("q (m o t) -> q m o t", m=4, t=4)
-            src = st[:, 0, :].rearrange("q (m t o) -> q m o t", m=4, t=4)
-            if eng == "scalar":
+        def regroup_w(n, on_scalar):
+            stage = w_stage[n]
+            dst = stage[:, 1, :].rearrange("q (m o t) -> q m o t", m=4, t=4)
+            src = stage[:, 0, :].rearrange("q (m t o) -> q m o t", m=4, t=4)
+            if on_scalar:
                 nc.scalar.copy(out=dst, in_=src)
-            elif eng == "gpsimd":
-                nc.gpsimd.tensor_scalar(out=dst, in0=src, scalar1=1.0, scalar2=0.0, op0=ALU.mult, op1=ALU.add)
             else:
                 nc.vector.tensor_copy(out=dst, in_=src)
 
-        def quant_w(vi):
-            v = VORDER[vi]
+        def quant_w(n):
+            v = ORDER[n]
             nc.vector.quantize_mx(
-                out=wcodes[:, v].rearrange("q m o -> q (m o)").bitcast(FP8X4),
-                scales=wscales[:, v].rearrange("q m o -> q (m o)"),
-                in_=wst[vi][:, 1, :],
+                out=w_codes[:, v].rearrange("q m o -> q (m o)").bitcast(FP8X4),
+                scales=w_scales[:, v].rearrange("q m o -> q (m o)"),
+                in_=w_stage[n][:, 1, :],
             )
 
-        gxs = {}
-        xts = {}
-        xcodes = {}
+        x_regrouped = {}
+        x_banks = {}
+        x_quantised = {}
 
-        def xt_bank(s, j):
-            g, c, bp = j // 4, (j // 2) % 2, j % 2
-            xf = xraws[s][:].bitcast(F32)
-            xt = psx.tile([P, 2, 2, P], F32, name="xt")
-            for bl in range(2):
+        def bank_of(j):
+            return j // 4, (j // 2) % 2, j % 2
+
+        def transpose_x(s, j):
+            g, c, nl = bank_of(j)
+            words = x_raw[s][:].bitcast(F32)
+            bank = ps_x.tile([P, 2, 2, P], F32, name="bank")
+            for h in range(2):
                 for u in range(2):
-                    lo = (2 * g + c) * 256 + u * P
-                    nc.tensor.transpose(xt[:, bl, u, :], xf[:, 2 * bp + bl, lo:lo + P], identf[:])
-            xts[(s, j)] = xt
+                    lo = (2 * g + c) * PASS_WORDS + u * P
+                    nc.tensor.transpose(bank[:, h, u, :], words[:, 2 * nl + h, lo:lo + P], ident_f32[:])
+            x_banks[(s, j)] = bank
 
-        def xe_bank(s, j, on_vector=False):
-            g, c, bp = j // 4, (j // 2) % 2, j % 2
-            if (s, g) not in gxs:
-                gxs[(s, g)] = xgr.tile([P, 2, 4 * 512], BF16, name="gx", align_bytes=64)
-            gxf = gxs[(s, g)][:].bitcast(F32)
-            dst = gxf[:, c, bp * 512:(bp + 1) * 512].rearrange("p (h r u) -> p h r u", h=2, u=2)
-            src = xts[(s, j)][:].rearrange("p h u r -> p h r u")
-            if on_vector:
-                nc.vector.tensor_copy(out=dst, in_=src)
-            else:
-                nc.scalar.copy(out=dst, in_=src)
+        def copy_out_x(s, j):
+            g, c, nl = bank_of(j)
+            if (s, g) not in x_regrouped:
+                x_regrouped[(s, g)] = x_grouped.tile([P, 2, 4 * PASS_COLS], BF16, name="grouped", align_bytes=64)
+            words = x_regrouped[(s, g)][:].bitcast(F32)
+            nc.scalar.copy(
+                out=words[:, c, nl * 2 * SEG:(nl + 1) * 2 * SEG].rearrange("p (h r u) -> p h r u", h=2, u=2),
+                in_=x_banks[(s, j)][:].rearrange("p h u r -> p h r u"),
+            )
 
         def quant_x(s, g):
-            codes = xq.tile([P, 1024], U32, name="codes", align_bytes=64)
-            scales = xq.tile([P, 1024], U8, name="scales", align_bytes=64)
+            codes = x_mx.tile([P, 2 * PASS_COLS], U32, name="codes", align_bytes=64)
+            scales = x_mx.tile([P, 2 * PASS_COLS], U8, name="scales", align_bytes=64)
             nc.vector.quantize_mx(
                 out=codes[:].bitcast(FP8X4),
                 scales=scales[:],
-                in_=gxs[(s, g)][:].rearrange("p a c -> p (a c)"),
+                in_=x_regrouped[(s, g)][:].rearrange("p a c -> p (a c)"),
             )
-            xcodes[(s, g)] = (codes, scales)
+            x_quantised[(s, g)] = (codes, scales)
 
-        ybs = {}
-        a0s = {}
-        ysbs = {}
+        y_banks = {}
+        y0_normed = {}
 
-        def mx(s, v):
+        def mx_passes(s, v):
             for g in range(G):
-                codes, scales = xcodes[(s, g)]
-                yb = psy.tile([P, 2 * SEG], F32, name="yb")
+                codes, scales = x_quantised[(s, g)]
+                y = ps_y.tile([P, PASS_COLS], F32, name="y")
                 for c in range(2):
                     nc.tensor.matmul_mx(
-                        out=yb[:],
-                        lhsT=wcodes[:, v, 2 * g + c, :].bitcast(FP8X4),
-                        lhsT_scale=wscales[:, v, 2 * g + c, :],
-                        rhs=codes[:, c * 512:(c + 1) * 512].bitcast(FP8X4),
-                        rhs_scale=scales[:, c * 512:(c + 1) * 512],
+                        out=y[:],
+                        lhsT=w_codes[:, v, 2 * g + c, :].bitcast(FP8X4),
+                        lhsT_scale=w_scales[:, v, 2 * g + c, :],
+                        rhs=codes[:, c * PASS_COLS:(c + 1) * PASS_COLS].bitcast(FP8X4),
+                        rhs_scale=scales[:, c * PASS_COLS:(c + 1) * PASS_COLS],
                         start=(c == 0),
                         stop=(c == 1),
                     )
-                ybs[(s, v, g)] = yb
+                y_banks[(s, v, g)] = y
 
-        def conv_init(eng, s, v, g, src):
+        def by_batch(y):
+            return y[:].rearrange("p (n c) -> p n c", n=2)
+
+        def by_parity(y):
+            return y[:].rearrange("p (n t r q) -> p n t r q", n=2, r=2, q=HW)
+
+        def odd_times(g, first, last):
+            return y4_odd[:, g, :, first * HW:last * HW].rearrange("p n (t q) -> p n t q", q=HW)
+
+        def first_tap(s, v, g):
             tcn = s % NCH
-            base = tcn * SEG
             i = v - 1
-            k = 2 * i + g
-            sh = HW * v
-            t0ap = tp[:, i, 0, g:g + 1]
+            shift = HW * v
             if tcn < NCH - 1:
-                pieces = [(0, SEG, cf)]
+                pieces = [(0, SEG, const_mid)]
             else:
-                pieces = [(0, SEG - 2 * sh, cf), (SEG - 2 * sh, SEG - sh, chi)]
-            for lo, hi, cst in pieces:
-                dst = acc[:, k, :, base + sh + lo:base + sh + hi]
-                if eng == "gpsimd":
-                    nc.gpsimd.tensor_scalar(
-                        out=dst, in0=src[:, :, lo:hi], scalar1=t0ap, scalar2=cst[:, i, g:g + 1],
-                        op0=ALU.mult, op1=ALU.add,
-                    )
-                elif eng == "vector":
-                    nc.vector.tensor_scalar(
-                        out=dst, in0=src[:, :, lo:hi], scalar1=t0ap, scalar2=cst[:, i, g:g + 1],
-                        op0=ALU.mult, op1=ALU.add,
-                    )
-                else:
-                    nc.scalar.activation(
-                        out=dst, in_=src[:, :, lo:hi], func=ACT.Identity, scale=t0ap, bias=cst[:, i, g:g + 1],
-                    )
+                pieces = [(0, SEG - 2 * shift, const_mid), (SEG - 2 * shift, SEG - shift, const_end)]
+            for lo, hi, constant in pieces:
+                at = tcn * SEG + shift
+                nc.scalar.activation(
+                    out=acc[:, 2 * i + g, :, at + lo:at + hi], in_=by_batch(y_banks[(s, v, g)])[:, :, lo:hi],
+                    func=ACT.Identity, scale=taps_scaled[:, i, 0, g:g + 1], bias=constant[:, i, g:g + 1],
+                )
 
-        def fp(s, v):
-            tcn = s % NCH
-            t0 = tcn * NH
+        def first_read(s, v):
+            t0 = (s % NCH) * NH
             if v == 0:
-                a0s[s] = a0p.tile([P, G, 2 * SEG], F32, name="a0")
+                y0_normed[s] = normed0.tile([P, G, PASS_COLS], F32, name="normed")
             for g in range(G):
-                yb = ybs[(s, v, g)]
                 if v == 0:
                     nc.scalar.activation(
-                        out=a0s[s][:, g, :], in_=yb[:], func=ACT.Identity,
-                        scale=sc[:, 0, g:g + 1], bias=cb[:, 0, g:g + 1],
+                        out=y0_normed[s][:, g, :], in_=y_banks[(s, v, g)][:], func=ACT.Identity,
+                        scale=bn_scale[:, 0, g:g + 1], bias=bn_const[:, 0, g:g + 1],
                     )
                 elif v == 4:
-                    yp = yb[:].rearrange("p (n t r q) -> p n t r q", n=2, r=2, q=HW)
-                    nc.scalar.copy(
-                        out=yo[:, g, :, t0 * HW:(t0 + NH) * HW].rearrange("p n (t q) -> p n t q", q=HW),
-                        in_=yp[:, :, :, 1, :],
-                    )
-                elif (v, g) in GP:
-                    ysb = gpp.tile([P, 2, SEG], F32, name="ysb")
-                    nc.scalar.copy(out=ysb[:], in_=yb[:].rearrange("p (n c) -> p n c", n=2))
-                    ysbs[(s, v, g)] = ysb
+                    nc.scalar.copy(out=odd_times(g, t0, t0 + NH), in_=by_parity(y_banks[(s, v, g)])[:, :, :, 1, :])
                 else:
-                    conv_init("vector" if (v, g) in FPD else "scalar", s, v, g, yb[:].rearrange("p (n c) -> p n c", n=2))
+                    first_tap(s, v, g)
 
-        def taps(s, v):
+        def other_reads(s, v):
             tcn = s % NCH
-            base = tcn * SEG
             t0 = tcn * NH
             if v == 0:
                 return
             if v == 4:
-                lo = 1 if tcn == 0 else 0
+                skip = 1 if tcn == 0 else 0
                 for g in range(G):
-                    yp = ybs[(s, v, g)][:].rearrange("p (n t r q) -> p n t r q", n=2, r=2, q=HW)
                     nc.vector.tensor_tensor(
-                        out=u4v[:, g, :, t0:t0 + NH, 0, :], in0=yp[:, :, :, 0, :],
-                        in1=yo[:, g, :, t0 * HW:(t0 + NH) * HW].rearrange("p n (t q) -> p n t q", q=HW),
-                        op=ALU.max,
+                        out=u4_by_group[:, g, :, t0:t0 + NH, 0, :], in0=by_parity(y_banks[(s, v, g)])[:, :, :, 0, :],
+                        in1=odd_times(g, t0, t0 + NH), op=ALU.max,
                     )
                 for g in range(G):
-                    yp = ybs[(s, v, g)][:].rearrange("p (n t r q) -> p n t r q", n=2, r=2, q=HW)
                     nc.vector.tensor_tensor(
-                        out=u4v[:, g, :, t0 + lo - 1:t0 + NH - 1, 1, :], in0=yp[:, :, lo:NH, 0, :],
-                        in1=yo[:, g, :, (t0 + lo - 1) * HW:(t0 + NH - 1) * HW].rearrange(
-                            "p n (t q) -> p n t q", q=HW),
-                        op=ALU.max,
+                        out=u4_by_group[:, g, :, t0 + skip - 1:t0 + NH - 1, 1, :],
+                        in0=by_parity(y_banks[(s, v, g)])[:, :, skip:NH, 0, :],
+                        in1=odd_times(g, t0 + skip - 1, t0 + NH - 1), op=ALU.max,
                     )
                 if tcn == NCH - 1:
                     nc.vector.tensor_copy(
-                        out=u4w[:, :, T // 2 - 1, 1, :],
-                        in_=yo[:].rearrange("p g n c -> p (g n) c")[:, :, (T // 2 - 1) * HW:(T // 2) * HW],
+                        out=u4_pairs[:, :, T // 2 - 1, 1, :],
+                        in_=y4_odd[:].rearrange("p g n c -> p (g n) c")[:, :, (T // 2 - 1) * HW:(T // 2) * HW],
                     )
                 return
             i = v - 1
-            sh = HW * v
-            lo = sh if tcn == 0 else 0
+            shift = HW * v
+            skip = shift if tcn == 0 else 0
             if tcn == 0:
                 for g in range(G):
                     nc.vector.tensor_scalar(
-                        out=acc[:, 2 * i + g, :, 0:sh], in0=zeros[:, :, 0:sh],
-                        scalar1=clo[:, i, g:g + 1], scalar2=None, op0=ALU.add,
+                        out=acc[:, 2 * i + g, :, 0:shift], in0=zeros[:, :, 0:shift],
+                        scalar1=const_start[:, i, g:g + 1], scalar2=None, op0=ALU.add,
                     )
-            for g in range(G):
-                if (v, g) in GP:
-                    k = 2 * i + g
-                    ysb = ysbs[(s, v, g)]
-                    conv_init("gpsimd", s, v, g, ysb[:])
-                    for j, a, z in ((1, 0, SEG), (2, lo, SEG)):
-                        off = base - (j - 1) * sh
-                        gt = gpp.tile([P, 2, SEG], F32, name="gt")
-                        nc.gpsimd.tensor_scalar(
-                            out=gt[:, :, a:z], in0=ysb[:, :, a:z], scalar1=tp[:, i, j, g:g + 1], scalar2=0.0,
-                            op0=ALU.mult, op1=ALU.add,
-                        )
-                        nc.gpsimd.tensor_tensor(
-                            out=acc[:, k, :, off + a:off + z], in0=acc[:, k, :, off + a:off + z],
-                            in1=gt[:, :, a:z], op=ALU.add,
-                        )
-            for j, a, z in ((1, 0, SEG), (2, lo, SEG)):
-                off = base - (j - 1) * sh
+            for j, lo in ((1, 0), (2, skip)):
+                at = tcn * SEG - (j - 1) * shift
                 for g in range(G):
-                    if (v, g) in GP:
-                        continue
-                    k = 2 * i + g
-                    yv = ybs[(s, v, g)][:].rearrange("p (n c) -> p n c", n=2)
+                    cells = acc[:, 2 * i + g, :, at + lo:at + SEG]
                     nc.vector.scalar_tensor_tensor(
-                        out=acc[:, k, :, off + a:off + z], in0=yv[:, :, a:z], scalar=tp[:, i, j, g:g + 1],
-                        in1=acc[:, k, :, off + a:off + z], op0=ALU.mult, op1=ALU.add,
+                        out=cells, in0=by_batch(y_banks[(s, v, g)])[:, :, lo:SEG], scalar=taps_scaled[:, i, j, g:g + 1],
+                        in1=cells, op0=ALU.mult, op1=ALU.add,
                     )
 
-        pls = {}
-        pts = {}
-        ots = {}
-        done = {}
+        pooled = {}
+        back_banks = {}
+        out_rows = {}
+        branches_done = {}
 
-        def affine4(s, g):
-            base = (s % NCH) * SEG
+        def norm4(s, g):
+            at = (s % NCH) * SEG
+            cells = u4[:, g, :, at:at + SEG]
             if g == 0:
                 nc.scalar.activation(
-                    out=u4[:, g, :, base:base + SEG], in_=u4[:, g, :, base:base + SEG], func=ACT.Identity,
-                    scale=sc[:, 4, g:g + 1], bias=cb[:, 4, g:g + 1],
+                    out=cells, in_=cells, func=ACT.Identity, scale=bn_scale[:, 4, g:g + 1], bias=bn_const[:, 4, g:g + 1],
                 )
             else:
                 nc.gpsimd.tensor_scalar(
-                    out=u4[:, g, :, base:base + SEG], in0=u4[:, g, :, base:base + SEG],
-                    scalar1=sc[:, 4, g:g + 1], scalar2=cb[:, 4, g:g + 1], op0=ALU.mult, op1=ALU.add,
+                    out=cells, in0=cells, scalar1=bn_scale[:, 4, g:g + 1], scalar2=bn_const[:, 4, g:g + 1],
+                    op0=ALU.mult, op1=ALU.add,
                 )
 
         def pool_pairs(s, v):
             t0 = (s % NCH) * NH
-            if s not in pls:
-                pls[s] = plp.tile([P, 2 * NV, SEG], F32, name="pl", tag="pl", align_bytes=64)
+            if s not in pooled:
+                pooled[s] = pooled_pool.tile([P, G * NV, SEG], F32, name="pooled", tag="pooled", align_bytes=64)
             if v == 0:
-                view = a0s[s][:].rearrange("p g (n t r q) -> p (g n) t r q", n=2, r=2, q=HW)
+                pairs = y0_normed[s][:].rearrange("p g (n t r q) -> p (g n) t r q", n=2, r=2, q=HW)
             elif v == 4:
-                view = u4w[:, :, t0:t0 + NH]
+                pairs = u4_pairs[:, :, t0:t0 + NH]
             else:
-                view = accv[:, 4 * (v - 1):4 * v, t0:t0 + NH]
+                pairs = acc_pairs[:, 4 * (v - 1):4 * v, t0:t0 + NH]
             nc.vector.tensor_tensor(
-                out=pls[s][:, 2 * v:2 * v + 2, :].rearrange("p g (n t q) -> p (g n) t q", n=2, q=HW),
-                in0=view[:, :, :, 0, :], in1=view[:, :, :, 1, :], op=ALU.max,
+                out=pooled[s][:, 2 * v:2 * v + 2, :].rearrange("p g (n t q) -> p (g n) t q", n=2, q=HW),
+                in0=pairs[:, :, :, 0, :], in1=pairs[:, :, :, 1, :], op=ALU.max,
             )
 
-        def ot_bank(s, v):
-            pt = pso.tile([P, 2, 2, P], F32, name="pt", tag="ot")
+        def transpose_back(s, v):
+            bank = ps_back.tile([P, 2, 2, P], F32, name="back", tag="back")
             for nl in range(2):
                 for g in range(G):
-                    nc.tensor.transpose(pt[:, nl, g, :], pls[s][:, 2 * v + g, nl * P:(nl + 1) * P], identf[:])
-            pts[(s, v)] = pt
+                    nc.tensor.transpose(bank[:, nl, g, :], pooled[s][:, 2 * v + g, nl * P:(nl + 1) * P], ident_f32[:])
+            back_banks[(s, v)] = bank
 
-        def oe_bank(s, v):
-            npair, tcn = divmod(s, NCH)
-            if s >= FINE_FROM:
-                otf = gpp.tile([P, 2, 2 * CB], F32, name="otf", bufs=NV)
-                dst = otf[:].rearrange("p n (o g) -> p n o g", g=2)
+        def relu_and_store(s, v):
+            pair, tcn = divmod(s, NCH)
+            by_branch = s >= STORE_BY_BRANCH_FROM
+            if by_branch:
+                small = out_small.tile([P, 2, OUT_V], F32, name="small")
+                dst = small[:]
             else:
-                if s not in ots:
-                    ots[s] = otp.tile([P, 2, 2 * NV * CB], F32, name="ot", tag="ot", align_bytes=64)
-                    done[s] = 0
-                dst = ots[s][:, :, v * 256:(v + 1) * 256].rearrange("p n (o g) -> p n o g", g=2)
-            src = pts[(s, v)][:].rearrange("p n g o -> p n o g")
-            if v in OE_DVE:
-                nc.vector.tensor_scalar_max(out=dst, in0=src, scalar1=0.0)
-            else:
-                nc.scalar.activation(out=dst, in_=src, func=ACT.Relu)
-            if s >= FINE_FROM:
+                if s not in out_rows:
+                    out_rows[s] = out_pool.tile([P, 2, NV * OUT_V], F32, name="out_rows", tag="out_rows", align_bytes=64)
+                    branches_done[s] = 0
+                dst = out_rows[s][:, :, v * OUT_V:(v + 1) * OUT_V]
+            nc.scalar.activation(
+                out=dst.rearrange("p n (o g) -> p n o g", g=2),
+                in_=back_banks[(s, v)][:].rearrange("p n g o -> p n o g"), func=ACT.Relu,
+            )
+            rows = [out[2 * pair + nl, tcn * NH:(tcn + 1) * NH].rearrange("t p q c -> (t p q) c") for nl in range(2)]
+            if by_branch:
                 for nl in range(2):
-                    nc.sync.dma_start(
-                        out=out[2 * npair + nl, tcn * NH:(tcn + 1) * NH].rearrange(
-                            "t p q c -> (t p q) c")[:, v * 256:(v + 1) * 256],
-                        in_=otf[:, nl, :],
-                    )
+                    nc.sync.dma_start(out=rows[nl][:, v * OUT_V:(v + 1) * OUT_V], in_=small[:, nl, :])
                 return
-            done[s] = done[s] + 1
-            if done[s] == NV:
+            branches_done[s] = branches_done[s] + 1
+            if branches_done[s] == NV:
                 for nl in range(2):
-                    nc.sync.dma_start(
-                        out=out[2 * npair + nl, tcn * NH:(tcn + 1) * NH].rearrange("t p q c -> (t p q) c"),
-                        in_=ots[s][:, nl, :],
-                    )
+                    nc.sync.dma_start(out=rows[nl], in_=out_rows[s][:, nl, :])
 
-        xt_at = {}
-        q_at = {}
-        ld_at = {}
+        def put(table, slot, item):
+            table[slot] = table.get(slot, []) + [item]
+
+        x_stage_at = {}
+        quant_at = {}
+        load_at = {}
+        norm4_at = {}
         pool_at = {}
-        ot_at = {}
-        de_at = {}
-        last_xt = {0: -1}
+        back_at = {}
+        x_stage_end = {0: -1}
         for c in range(1, NSTEP):
-            first = NV * (c - 1) - XAHEAD[c]
-            for q in range(4):
-                xt_at[first + q] = xt_at.get(first + q, []) + [(c, q)]
-            q_at[first + 2] = q_at.get(first + 2, []) + [(c, 0)]
-            q_at[first + 3] = q_at.get(first + 3, []) + [(c, 1)]
-            last_xt[c] = first + 3
+            first = NV * (c - 1) - X_AHEAD[c]
+            for pair_of_banks in range(4):
+                put(x_stage_at, first + pair_of_banks, (c, pair_of_banks))
+            put(quant_at, first + 2, (c, 0))
+            put(quant_at, first + 3, (c, 1))
+            x_stage_end[c] = first + 3
         for c in range(2, NSTEP):
-            at = max(0, last_xt[c - 2] + 1)
-            ld_at[at] = ld_at.get(at, []) + [c]
-        for r in range(NU):
-            s_r, vi_r = divmod(r, NV)
-            v_r = VORDER[vi_r]
-            dep = r + NV if (s_r < NSTEP - 1 and v_r != 0) else r
-            at = dep + LAG[v_r]
-            pool_at[at] = pool_at.get(at, []) + [(s_r, v_r)]
-            ot_at[at + OLAG] = ot_at.get(at + OLAG, []) + [(s_r, v_r)]
-            if v_r == 4:
-                de_at[dep] = de_at.get(dep, []) + [s_r]
+            put(load_at, max(0, x_stage_end[c - 2] + 1), c)
+        for unit in range(NU):
+            s, v = unit // NV, ORDER[unit % NV]
+            complete = unit + NV if (s < NSTEP - 1 and v != 0) else unit
+            put(pool_at, complete + POOL_LAG[v], (s, v))
+            put(back_at, complete + POOL_LAG[v] + BACK_LAG, (s, v))
+            if v == 4:
+                put(norm4_at, complete, s)
 
-        regroup_w(0, "vector")
-        regroup_w(1, "scalar")
-        regroup_w(2, "vector")
+        regroup_w(0, False)
+        regroup_w(1, True)
+        regroup_w(2, False)
         quant_w(0)
         quant_w(1)
         quant_w(2)
-        ptp = pso.tile([P, P], BF16, name="ptp", tag="ot")
-        nc.tensor.transpose(ptp[:], praw[:], identb[:])
-        par = const.tile([P, 68], F32, name="par")
-        nc.vector.tensor_copy(out=par[:], in_=ptp[:, 0:68])
-        bv = par[:, 0:10].rearrange("p (v g) -> p v g", g=2)
-        dwv = par[:, 10:28].rearrange("p (i j g) -> p i j g", j=3, g=2)
-        bnv = par[:, 28:68].rearrange("p (v k g) -> p v k g", k=4, g=2)
 
-        ve = const.tile([P, NV, G], F32, name="ve")
-        rs = const.tile([P, NV, G], F32, name="rs")
-        tmp = const.tile([P, NV, G], F32, name="tmp")
-        sc = const.tile([P, NV, G], F32, name="sc")
-        c0 = const.tile([P, NV, G], F32, name="c0")
-        cb = const.tile([P, NV, G], F32, name="cb")
-        nc.vector.tensor_scalar_add(out=ve[:], in0=bnv[:, :, 3, :], scalar1=EPS)
-        nc.scalar.sqrt(out=rs[:], in_=ve[:])
-        nc.vector.reciprocal(out=rs[:], in_=rs[:])
-        nc.vector.tensor_mul(out=tmp[:], in0=rs[:], in1=rs[:])
-        nc.vector.tensor_mul(out=tmp[:], in0=tmp[:], in1=ve[:])
-        nc.vector.tensor_scalar(out=tmp[:], in0=tmp[:], scalar1=-0.5, scalar2=1.5, op0=ALU.mult, op1=ALU.add)
-        nc.vector.tensor_mul(out=rs[:], in0=rs[:], in1=tmp[:])
-        nc.vector.tensor_mul(out=sc[:], in0=rs[:], in1=bnv[:, :, 0, :])
-        nc.vector.tensor_mul(out=tmp[:], in0=sc[:], in1=bnv[:, :, 2, :])
-        nc.vector.tensor_sub(out=c0[:], in0=bnv[:, :, 1, :], in1=tmp[:])
-        nc.vector.tensor_mul(out=tmp[:], in0=sc[:], in1=bv)
-        nc.vector.tensor_add(out=cb[:], in0=c0[:], in1=tmp[:])
-        tp = const.tile([P, 3, 3, G], F32, name="tp")
-        tb = const.tile([P, 3, 3, G], F32, name="tb")
-        for j in range(3):
-            nc.vector.tensor_mul(out=tp[:, :, j, :], in0=dwv[:, :, j, :], in1=sc[:, 1:4, :])
-        for j in range(3):
-            nc.vector.tensor_mul(out=tb[:, :, j, :], in0=tp[:, :, j, :], in1=bv[:, 1:4, :])
-        chi = const.tile([P, 3, G], F32, name="chi")
-        cf = const.tile([P, 3, G], F32, name="cf")
-        clo = const.tile([P, 3, G], F32, name="clo")
-        nc.vector.tensor_add(out=clo[:], in0=c0[:, 1:4, :], in1=tb[:, :, 1, :])
-        nc.vector.tensor_add(out=chi[:], in0=clo[:], in1=tb[:, :, 0, :])
-        nc.vector.tensor_add(out=cf[:], in0=chi[:], in1=tb[:, :, 2, :])
-        nc.vector.tensor_add(out=clo[:], in0=clo[:], in1=tb[:, :, 2, :])
+        params_t = ps_back.tile([P, P], BF16, name="params_t", tag="back")
+        nc.tensor.transpose(params_t[:], param_rows[:], ident_bf16[:])
+        params = const.tile([P, N_PARAM_ROWS], F32, name="params")
+        nc.vector.tensor_copy(out=params[:], in_=params_t[:, 0:N_PARAM_ROWS])
+        bias = params[:, 0:ROW_DW].rearrange("p (v g) -> p v g", g=2)
+        taps = params[:, ROW_DW:ROW_BN].rearrange("p (i j g) -> p i j g", j=3, g=2)
+        bn_rows = params[:, ROW_BN:N_PARAM_ROWS].rearrange("p (v k g) -> p v k g", k=4, g=2)
 
-        regroup_w(3, "vector")
+        var_eps = const.tile([P, NV, G], F32, name="var_eps")
+        rstd = const.tile([P, NV, G], F32, name="rstd")
+        work = const.tile([P, NV, G], F32, name="work")
+        bn_scale = const.tile([P, NV, G], F32, name="bn_scale")
+        bn_shift = const.tile([P, NV, G], F32, name="bn_shift")
+        bn_const = const.tile([P, NV, G], F32, name="bn_const")
+        nc.vector.tensor_scalar_add(out=var_eps[:], in0=bn_rows[:, :, 3, :], scalar1=EPS)
+        nc.scalar.sqrt(out=rstd[:], in_=var_eps[:])
+        nc.vector.reciprocal(out=rstd[:], in_=rstd[:])
+        nc.vector.tensor_mul(out=work[:], in0=rstd[:], in1=rstd[:])
+        nc.vector.tensor_mul(out=work[:], in0=work[:], in1=var_eps[:])
+        nc.vector.tensor_scalar(out=work[:], in0=work[:], scalar1=-0.5, scalar2=1.5, op0=ALU.mult, op1=ALU.add)
+        nc.vector.tensor_mul(out=rstd[:], in0=rstd[:], in1=work[:])
+        nc.vector.tensor_mul(out=bn_scale[:], in0=rstd[:], in1=bn_rows[:, :, 0, :])
+        nc.vector.tensor_mul(out=work[:], in0=bn_scale[:], in1=bn_rows[:, :, 2, :])
+        nc.vector.tensor_sub(out=bn_shift[:], in0=bn_rows[:, :, 1, :], in1=work[:])
+        nc.vector.tensor_mul(out=work[:], in0=bn_scale[:], in1=bias)
+        nc.vector.tensor_add(out=bn_const[:], in0=bn_shift[:], in1=work[:])
+        taps_scaled = const.tile([P, 3, 3, G], F32, name="taps_scaled")
+        tap_bias = const.tile([P, 3, 3, G], F32, name="tap_bias")
+        for j in range(3):
+            nc.vector.tensor_mul(out=taps_scaled[:, :, j, :], in0=taps[:, :, j, :], in1=bn_scale[:, 1:4, :])
+        for j in range(3):
+            nc.vector.tensor_mul(out=tap_bias[:, :, j, :], in0=taps_scaled[:, :, j, :], in1=bias[:, 1:4, :])
+        const_end = const.tile([P, 3, G], F32, name="const_end")
+        const_mid = const.tile([P, 3, G], F32, name="const_mid")
+        const_start = const.tile([P, 3, G], F32, name="const_start")
+        nc.vector.tensor_add(out=const_start[:], in0=bn_shift[:, 1:4, :], in1=tap_bias[:, :, 1, :])
+        nc.vector.tensor_add(out=const_end[:], in0=const_start[:], in1=tap_bias[:, :, 0, :])
+        nc.vector.tensor_add(out=const_mid[:], in0=const_end[:], in1=tap_bias[:, :, 2, :])
+        nc.vector.tensor_add(out=const_start[:], in0=const_start[:], in1=tap_bias[:, :, 2, :])
+
+        regroup_w(3, False)
         for j in range(8):
-            xt_bank(0, j)
-            xe_bank(0, j)
+            transpose_x(0, j)
+            copy_out_x(0, j)
             if j == 5:
                 quant_x(0, 0)
                 quant_w(3)
         quant_x(0, 1)
 
-        for u in range(NU + 12):
-            s, vi = divmod(u, NV)
-            live = u < NU
-            for c in ld_at.get(u, []):
+        last_slot = max(back_at)
+        for slot in range(last_slot + 1):
+            s, v = slot // NV, ORDER[slot % NV]
+            has_unit = slot < NU
+            x_pairs = x_stage_at.get(slot, [])
+            for c in load_at.get(slot, []):
                 load_x(c)
-            if live:
-                v = VORDER[vi]
-                mx(s, v)
-            for c, q in xt_at.get(u, [])[:1]:
-                xt_bank(c, 2 * q)
-                xt_bank(c, 2 * q + 1)
-            for s_r, v_r in ot_at.get(u, []):
-                ot_bank(s_r, v_r)
-            if live:
-                fp(s, v)
-            for s_r in de_at.get(u - 1, []):
-                affine4(s_r, 0)
-            if live:
-                taps(s, v)
-            for s_r in de_at.get(u, []):
-                affine4(s_r, 1)
-            for s_r, v_r in pool_at.get(u, []):
-                pool_pairs(s_r, v_r)
-            for n_pair, (c, q) in enumerate(xt_at.get(u, [])):
-                if n_pair > 0:
-                    xt_bank(c, 2 * q)
-                    xt_bank(c, 2 * q + 1)
-                xe_bank(c, 2 * q)
-                xe_bank(c, 2 * q + 1)
-            for s_r, v_r in ot_at.get(u, []):
-                oe_bank(s_r, v_r)
-            for c, g in q_at.get(u, []):
+            if has_unit:
+                mx_passes(s, v)
+            for c, pair_of_banks in x_pairs[:1]:
+                transpose_x(c, 2 * pair_of_banks)
+                transpose_x(c, 2 * pair_of_banks + 1)
+            for chunk, branch in back_at.get(slot, []):
+                transpose_back(chunk, branch)
+            if has_unit:
+                first_read(s, v)
+            for chunk in norm4_at.get(slot - 1, []):
+                norm4(chunk, 0)
+            if has_unit:
+                other_reads(s, v)
+            for chunk in norm4_at.get(slot, []):
+                norm4(chunk, 1)
+            for chunk, branch in pool_at.get(slot, []):
+                pool_pairs(chunk, branch)
+            for n, (c, pair_of_banks) in enumerate(x_pairs):
+                if n > 0:
+                    transpose_x(c, 2 * pair_of_banks)
+                    transpose_x(c, 2 * pair_of_banks + 1)
+                copy_out_x(c, 2 * pair_of_banks)
+                copy_out_x(c, 2 * pair_of_banks + 1)
+            for chunk, branch in back_at.get(slot, []):
+                relu_and_store(chunk, branch)
+            for c, g in quant_at.get(slot, []):
                 quant_x(c, g)
-            if u == 0:
-                regroup_w(4, "vector")
-            if u == 1:
+            if slot == 0:
+                regroup_w(4, False)
+            if slot == 1:
                 quant_w(4)

from contextlib import ExitStack

import concourse.mybir as mybir
from concourse.masks import make_identity

F32 = mybir.dt.float32
BF16 = mybir.dt.bfloat16
U32 = mybir.dt.uint32
U8 = mybir.dt.uint8
FP8X4 = mybir.dt.float8_e4m3fn_x4
ALU = mybir.AluOpType
ACT = mybir.ActivationFunctionType

P = 128
B, T, HW, G, K, CB, NV = 4, 64, 16, 2, 1024, 128, 5
EPS = 1e-3
FLOPS = 2 * B * T * HW * G * K * NV * CB

TC = 16
NCH = T // TC
SEG = TC * HW
NH = TC // 2
NSTEP = (B // 2) * NCH
PASS_COLS = 2 * SEG
OUT_V = G * CB

ORDER = (4, 3, 2, 1, 0)
NU = NSTEP * NV
X_AHEAD = (0, 0, 2, 3, 3, 3, 3, 3)
POOL_LAG = {0: 1, 1: 1, 2: 1, 3: 1, 4: 2}
BACK_LAG = 2
STORE_BY_BRANCH_FROM = NSTEP - 2
ROW_DW = NV * G
ROW_BN = ROW_DW + 3 * 3 * G
N_PARAM_ROWS = ROW_BN + NV * 4 * G
PASS_WORDS = 256


def tile_timeception_pa_t_kernel(tc, x, w, b, dw, bn, out):
    nc = tc.nc
    with ExitStack() as ctx:
        ctx.enter_context(tc.manual_schedule())
        const = ctx.enter_context(tc.tile_pool(name="const", bufs=1))
        keep = ctx.enter_context(tc.tile_pool(name="keep", bufs=1))
        x_in = ctx.enter_context(tc.tile_pool(name="x_in", bufs=2))
        x_grouped = ctx.enter_context(tc.tile_pool(name="x_grouped", bufs=2))
        x_mx = ctx.enter_context(tc.tile_pool(name="x_mx", bufs=4))
        normed0 = ctx.enter_context(tc.tile_pool(name="normed0", bufs=3))
        out_small = ctx.enter_context(tc.tile_pool(name="out_small", bufs=2 * NV))
        pooled_pool = ctx.enter_context(tc.tile_pool(name="pooled_pool", bufs=2))
        out_pool = ctx.enter_context(tc.tile_pool(name="out_pool", bufs=2))
        ps_x = ctx.enter_context(tc.psum_pool(name="ps_x", bufs=2))
        ps_y = ctx.enter_context(tc.psum_pool(name="ps_y", bufs=4))
        ps_back = ctx.enter_context(tc.psum_pool(name="ps_back", bufs=2))

        x_raw = {}

        def load_x(s):
            pair, tcn = divmod(s, NCH)
            raw = x_in.tile([P, 4, G * K], BF16, name="raw")
            for nl in range(2):
                src = x[2 * pair + nl, tcn * TC:(tcn + 1) * TC]
                nc.sync.dma_start(
                    out=raw[:, 2 * nl:2 * nl + 2, :],
                    in_=src.rearrange("(h t) p q c -> (t p q) h c", h=2),
                )
            x_raw[s] = raw

        w_stage = {}

        def load_w(n):
            pool, tag = (pooled_pool, "pooled") if n % 2 == 0 else (out_pool, "out_rows")
            stage = pool.tile([P, 2, 16 * P], BF16, name="stage", tag=tag, align_bytes=64)
            nc.sync.dma_start(
                out=stage[:, 0, :].rearrange("q (a f) -> q a f", f=2 * P),
                in_=w[ORDER[n]].rearrange("g (a q e) o -> q (g a) (e o)", q=P, e=2),
            )
            w_stage[n] = stage

        param_rows = const.tile([P, P], BF16, name="param_rows")
        nc.vector.memset(param_rows[:], 0.0)
        nc.sync.dma_start(out=param_rows[0:ROW_DW, :], in_=b.rearrange("v g o -> (v g) o"))
        nc.sync.dma_start(out=param_rows[ROW_DW:ROW_BN, :], in_=dw.rearrange("i j g o -> (i j g) o"))
        nc.sync.dma_start(out=param_rows[ROW_BN:N_PARAM_ROWS, :], in_=bn.rearrange("v k g o -> (v k g) o"))
        load_w(0)
        load_w(1)
        load_w(2)
        load_x(0)
        load_w(3)
        load_w(4)
        load_x(1)
        ident_f32 = const.tile([P, P], F32, name="ident_f32")
        make_identity(nc, ident_f32[:])
        ident_bf16 = const.tile([P, P], BF16, name="ident_bf16")
        make_identity(nc, ident_bf16[:])
        zeros = const.tile([P, 2, 3 * HW], F32, name="zeros")
        nc.vector.memset(zeros[:], 0.0)

        w_codes = keep.tile([P, NV, 4, P], U32, name="w_codes", align_bytes=64)
        w_scales = keep.tile([P, NV, 4, P], U8, name="w_scales", align_bytes=64)
        acc = keep.tile([P, 6, 2, T * HW], F32, name="acc")
        u4 = keep.tile([P, G, 2, T * HW], F32, name="u4")
        y4_odd = keep.tile([P, G, 2, T * HW // 2], F32, name="y4_odd")
        acc_pairs = acc[:].rearrange("p k n (t r q) -> p (k n) t r q", r=2, q=HW)
        u4_by_group = u4[:].rearrange("p g n (t r q) -> p g n t r q", r=2, q=HW)
        u4_pairs = u4[:].rearrange("p g n (t r q) -> p (g n) t r q", r=2, q=HW)

        def regroup_w(n, on_scalar):
            stage = w_stage[n]
            dst = stage[:, 1, :].rearrange("q (m o t) -> q m o t", m=4, t=4)
            src = stage[:, 0, :].rearrange("q (m t o) -> q m o t", m=4, t=4)
            if on_scalar:
                nc.scalar.copy(out=dst, in_=src)
            else:
                nc.vector.tensor_copy(out=dst, in_=src)

        def quant_w(n):
            v = ORDER[n]
            nc.vector.quantize_mx(
                out=w_codes[:, v].rearrange("q m o -> q (m o)").bitcast(FP8X4),
                scales=w_scales[:, v].rearrange("q m o -> q (m o)"),
                in_=w_stage[n][:, 1, :],
            )

        x_regrouped = {}
        x_banks = {}
        x_quantised = {}

        def bank_of(j):
            return j // 4, (j // 2) % 2, j % 2

        def transpose_x(s, j):
            g, c, nl = bank_of(j)
            words = x_raw[s][:].bitcast(F32)
            bank = ps_x.tile([P, 2, 2, P], F32, name="bank")
            for h in range(2):
                for u in range(2):
                    lo = (2 * g + c) * PASS_WORDS + u * P
                    nc.tensor.transpose(bank[:, h, u, :], words[:, 2 * nl + h, lo:lo + P], ident_f32[:])
            x_banks[(s, j)] = bank

        def copy_out_x(s, j):
            g, c, nl = bank_of(j)
            if (s, g) not in x_regrouped:
                x_regrouped[(s, g)] = x_grouped.tile([P, 2, 4 * PASS_COLS], BF16, name="grouped", align_bytes=64)
            words = x_regrouped[(s, g)][:].bitcast(F32)
            nc.scalar.copy(
                out=words[:, c, nl * 2 * SEG:(nl + 1) * 2 * SEG].rearrange("p (h r u) -> p h r u", h=2, u=2),
                in_=x_banks[(s, j)][:].rearrange("p h u r -> p h r u"),
            )

        def quant_x(s, g):
            codes = x_mx.tile([P, 2 * PASS_COLS], U32, name="codes", align_bytes=64)
            scales = x_mx.tile([P, 2 * PASS_COLS], U8, name="scales", align_bytes=64)
            nc.vector.quantize_mx(
                out=codes[:].bitcast(FP8X4),
                scales=scales[:],
                in_=x_regrouped[(s, g)][:].rearrange("p a c -> p (a c)"),
            )
            x_quantised[(s, g)] = (codes, scales)

        y_banks = {}
        y0_normed = {}

        def mx_passes(s, v):
            for g in range(G):
                codes, scales = x_quantised[(s, g)]
                y = ps_y.tile([P, PASS_COLS], F32, name="y")
                for c in range(2):
                    nc.tensor.matmul_mx(
                        out=y[:],
                        lhsT=w_codes[:, v, 2 * g + c, :].bitcast(FP8X4),
                        lhsT_scale=w_scales[:, v, 2 * g + c, :],
                        rhs=codes[:, c * PASS_COLS:(c + 1) * PASS_COLS].bitcast(FP8X4),
                        rhs_scale=scales[:, c * PASS_COLS:(c + 1) * PASS_COLS],
                        start=(c == 0),
                        stop=(c == 1),
                    )
                y_banks[(s, v, g)] = y

        def by_batch(y):
            return y[:].rearrange("p (n c) -> p n c", n=2)

        def by_parity(y):
            return y[:].rearrange("p (n t r q) -> p n t r q", n=2, r=2, q=HW)

        def odd_times(g, first, last):
            return y4_odd[:, g, :, first * HW:last * HW].rearrange("p n (t q) -> p n t q", q=HW)

        def first_tap(s, v, g):
            tcn = s % NCH
            i = v - 1
            shift = HW * v
            if tcn < NCH - 1:
                pieces = [(0, SEG, const_mid)]
            else:
                pieces = [(0, SEG - 2 * shift, const_mid), (SEG - 2 * shift, SEG - shift, const_end)]
            for lo, hi, constant in pieces:
                at = tcn * SEG + shift
                nc.scalar.activation(
                    out=acc[:, 2 * i + g, :, at + lo:at + hi], in_=by_batch(y_banks[(s, v, g)])[:, :, lo:hi],
                    func=ACT.Identity, scale=taps_scaled[:, i, 0, g:g + 1], bias=constant[:, i, g:g + 1],
                )

        def first_read(s, v):
            t0 = (s % NCH) * NH
            if v == 0:
                y0_normed[s] = normed0.tile([P, G, PASS_COLS], F32, name="normed")
            for g in range(G):
                if v == 0:
                    nc.scalar.activation(
                        out=y0_normed[s][:, g, :], in_=y_banks[(s, v, g)][:], func=ACT.Identity,
                        scale=bn_scale[:, 0, g:g + 1], bias=bn_const[:, 0, g:g + 1],
                    )
                elif v == 4:
                    nc.scalar.copy(out=odd_times(g, t0, t0 + NH), in_=by_parity(y_banks[(s, v, g)])[:, :, :, 1, :])
                else:
                    first_tap(s, v, g)

        def other_reads(s, v):
            tcn = s % NCH
            t0 = tcn * NH
            if v == 0:
                return
            if v == 4:
                skip = 1 if tcn == 0 else 0
                for g in range(G):
                    nc.vector.tensor_tensor(
                        out=u4_by_group[:, g, :, t0:t0 + NH, 0, :], in0=by_parity(y_banks[(s, v, g)])[:, :, :, 0, :],
                        in1=odd_times(g, t0, t0 + NH), op=ALU.max,
                    )
                for g in range(G):
                    nc.vector.tensor_tensor(
                        out=u4_by_group[:, g, :, t0 + skip - 1:t0 + NH - 1, 1, :],
                        in0=by_parity(y_banks[(s, v, g)])[:, :, skip:NH, 0, :],
                        in1=odd_times(g, t0 + skip - 1, t0 + NH - 1), op=ALU.max,
                    )
                if tcn == NCH - 1:
                    nc.vector.tensor_copy(
                        out=u4_pairs[:, :, T // 2 - 1, 1, :],
                        in_=y4_odd[:].rearrange("p g n c -> p (g n) c")[:, :, (T // 2 - 1) * HW:(T // 2) * HW],
                    )
                return
            i = v - 1
            shift = HW * v
            skip = shift if tcn == 0 else 0
            if tcn == 0:
                for g in range(G):
                    nc.vector.tensor_scalar(
                        out=acc[:, 2 * i + g, :, 0:shift], in0=zeros[:, :, 0:shift],
                        scalar1=const_start[:, i, g:g + 1], scalar2=None, op0=ALU.add,
                    )
            for j, lo in ((1, 0), (2, skip)):
                at = tcn * SEG - (j - 1) * shift
                for g in range(G):
                    cells = acc[:, 2 * i + g, :, at + lo:at + SEG]
                    nc.vector.scalar_tensor_tensor(
                        out=cells, in0=by_batch(y_banks[(s, v, g)])[:, :, lo:SEG], scalar=taps_scaled[:, i, j, g:g + 1],
                        in1=cells, op0=ALU.mult, op1=ALU.add,
                    )

        pooled = {}
        back_banks = {}
        out_rows = {}
        branches_done = {}

        def norm4(s, g):
            at = (s % NCH) * SEG
            cells = u4[:, g, :, at:at + SEG]
            if g == 0:
                nc.scalar.activation(
                    out=cells, in_=cells, func=ACT.Identity, scale=bn_scale[:, 4, g:g + 1], bias=bn_const[:, 4, g:g + 1],
                )
            else:
                nc.gpsimd.tensor_scalar(
                    out=cells, in0=cells, scalar1=bn_scale[:, 4, g:g + 1], scalar2=bn_const[:, 4, g:g + 1],
                    op0=ALU.mult, op1=ALU.add,
                )

        def pool_pairs(s, v):
            t0 = (s % NCH) * NH
            if s not in pooled:
                pooled[s] = pooled_pool.tile([P, G * NV, SEG], F32, name="pooled", tag="pooled", align_bytes=64)
            if v == 0:
                pairs = y0_normed[s][:].rearrange("p g (n t r q) -> p (g n) t r q", n=2, r=2, q=HW)
            elif v == 4:
                pairs = u4_pairs[:, :, t0:t0 + NH]
            else:
                pairs = acc_pairs[:, 4 * (v - 1):4 * v, t0:t0 + NH]
            nc.vector.tensor_tensor(
                out=pooled[s][:, 2 * v:2 * v + 2, :].rearrange("p g (n t q) -> p (g n) t q", n=2, q=HW),
                in0=pairs[:, :, :, 0, :], in1=pairs[:, :, :, 1, :], op=ALU.max,
            )

        def transpose_back(s, v):
            bank = ps_back.tile([P, 2, 2, P], F32, name="back", tag="back")
            for nl in range(2):
                for g in range(G):
                    nc.tensor.transpose(bank[:, nl, g, :], pooled[s][:, 2 * v + g, nl * P:(nl + 1) * P], ident_f32[:])
            back_banks[(s, v)] = bank

        def relu_and_store(s, v):
            pair, tcn = divmod(s, NCH)
            by_branch = s >= STORE_BY_BRANCH_FROM
            if by_branch:
                small = out_small.tile([P, 2, OUT_V], F32, name="small")
                dst = small[:]
            else:
                if s not in out_rows:
                    out_rows[s] = out_pool.tile([P, 2, NV * OUT_V], F32, name="out_rows", tag="out_rows", align_bytes=64)
                    branches_done[s] = 0
                dst = out_rows[s][:, :, v * OUT_V:(v + 1) * OUT_V]
            nc.scalar.activation(
                out=dst.rearrange("p n (o g) -> p n o g", g=2),
                in_=back_banks[(s, v)][:].rearrange("p n g o -> p n o g"), func=ACT.Relu,
            )
            rows = [out[2 * pair + nl, tcn * NH:(tcn + 1) * NH].rearrange("t p q c -> (t p q) c") for nl in range(2)]
            if by_branch:
                for nl in range(2):
                    nc.sync.dma_start(out=rows[nl][:, v * OUT_V:(v + 1) * OUT_V], in_=small[:, nl, :])
                return
            branches_done[s] = branches_done[s] + 1
            if branches_done[s] == NV:
                for nl in range(2):
                    nc.sync.dma_start(out=rows[nl], in_=out_rows[s][:, nl, :])

        def put(table, slot, item):
            table[slot] = table.get(slot, []) + [item]

        x_stage_at = {}
        quant_at = {}
        load_at = {}
        norm4_at = {}
        pool_at = {}
        back_at = {}
        x_stage_end = {0: -1}
        for c in range(1, NSTEP):
            first = NV * (c - 1) - X_AHEAD[c]
            for pair_of_banks in range(4):
                put(x_stage_at, first + pair_of_banks, (c, pair_of_banks))
            put(quant_at, first + 2, (c, 0))
            put(quant_at, first + 3, (c, 1))
            x_stage_end[c] = first + 3
        for c in range(2, NSTEP):
            put(load_at, max(0, x_stage_end[c - 2] + 1), c)
        for unit in range(NU):
            s, v = unit // NV, ORDER[unit % NV]
            complete = unit + NV if (s < NSTEP - 1 and v != 0) else unit
            put(pool_at, complete + POOL_LAG[v], (s, v))
            put(back_at, complete + POOL_LAG[v] + BACK_LAG, (s, v))
            if v == 4:
                put(norm4_at, complete, s)

        regroup_w(0, False)
        regroup_w(1, True)
        regroup_w(2, False)
        quant_w(0)
        quant_w(1)
        quant_w(2)

        params_t = ps_back.tile([P, P], BF16, name="params_t", tag="back")
        nc.tensor.transpose(params_t[:], param_rows[:], ident_bf16[:])
        params = const.tile([P, N_PARAM_ROWS], F32, name="params")
        nc.vector.tensor_copy(out=params[:], in_=params_t[:, 0:N_PARAM_ROWS])
        bias = params[:, 0:ROW_DW].rearrange("p (v g) -> p v g", g=2)
        taps = params[:, ROW_DW:ROW_BN].rearrange("p (i j g) -> p i j g", j=3, g=2)
        bn_rows = params[:, ROW_BN:N_PARAM_ROWS].rearrange("p (v k g) -> p v k g", k=4, g=2)

        var_eps = const.tile([P, NV, G], F32, name="var_eps")
        rstd = const.tile([P, NV, G], F32, name="rstd")
        work = const.tile([P, NV, G], F32, name="work")
        bn_scale = const.tile([P, NV, G], F32, name="bn_scale")
        bn_shift = const.tile([P, NV, G], F32, name="bn_shift")
        bn_const = const.tile([P, NV, G], F32, name="bn_const")
        nc.vector.tensor_scalar_add(out=var_eps[:], in0=bn_rows[:, :, 3, :], scalar1=EPS)
        nc.scalar.sqrt(out=rstd[:], in_=var_eps[:])
        nc.vector.reciprocal(out=rstd[:], in_=rstd[:])
        nc.vector.tensor_mul(out=work[:], in0=rstd[:], in1=rstd[:])
        nc.vector.tensor_mul(out=work[:], in0=work[:], in1=var_eps[:])
        nc.vector.tensor_scalar(out=work[:], in0=work[:], scalar1=-0.5, scalar2=1.5, op0=ALU.mult, op1=ALU.add)
        nc.vector.tensor_mul(out=rstd[:], in0=rstd[:], in1=work[:])
        nc.vector.tensor_mul(out=bn_scale[:], in0=rstd[:], in1=bn_rows[:, :, 0, :])
        nc.vector.tensor_mul(out=work[:], in0=bn_scale[:], in1=bn_rows[:, :, 2, :])
        nc.vector.tensor_sub(out=bn_shift[:], in0=bn_rows[:, :, 1, :], in1=work[:])
        nc.vector.tensor_mul(out=work[:], in0=bn_scale[:], in1=bias)
        nc.vector.tensor_add(out=bn_const[:], in0=bn_shift[:], in1=work[:])
        taps_scaled = const.tile([P, 3, 3, G], F32, name="taps_scaled")
        tap_bias = const.tile([P, 3, 3, G], F32, name="tap_bias")
        for j in range(3):
            nc.vector.tensor_mul(out=taps_scaled[:, :, j, :], in0=taps[:, :, j, :], in1=bn_scale[:, 1:4, :])
        for j in range(3):
            nc.vector.tensor_mul(out=tap_bias[:, :, j, :], in0=taps_scaled[:, :, j, :], in1=bias[:, 1:4, :])
        const_end = const.tile([P, 3, G], F32, name="const_end")
        const_mid = const.tile([P, 3, G], F32, name="const_mid")
        const_start = const.tile([P, 3, G], F32, name="const_start")
        nc.vector.tensor_add(out=const_start[:], in0=bn_shift[:, 1:4, :], in1=tap_bias[:, :, 1, :])
        nc.vector.tensor_add(out=const_end[:], in0=const_start[:], in1=tap_bias[:, :, 0, :])
        nc.vector.tensor_add(out=const_mid[:], in0=const_end[:], in1=tap_bias[:, :, 2, :])
        nc.vector.tensor_add(out=const_start[:], in0=const_start[:], in1=tap_bias[:, :, 2, :])

        regroup_w(3, False)
        for j in range(8):
            transpose_x(0, j)
            copy_out_x(0, j)
            if j == 5:
                quant_x(0, 0)
                quant_w(3)
        quant_x(0, 1)

        last_slot = max(back_at)
        for slot in range(last_slot + 1):
            s, v = slot // NV, ORDER[slot % NV]
            has_unit = slot < NU
            x_pairs = x_stage_at.get(slot, [])
            for c in load_at.get(slot, []):
                load_x(c)
            if has_unit:
                mx_passes(s, v)
            for c, pair_of_banks in x_pairs[:1]:
                transpose_x(c, 2 * pair_of_banks)
                transpose_x(c, 2 * pair_of_banks + 1)
            for chunk, branch in back_at.get(slot, []):
                transpose_back(chunk, branch)
            if has_unit:
                first_read(s, v)
            for chunk in norm4_at.get(slot - 1, []):
                norm4(chunk, 0)
            if has_unit:
                other_reads(s, v)
            for chunk in norm4_at.get(slot, []):
                norm4(chunk, 1)
            for chunk, branch in pool_at.get(slot, []):
                pool_pairs(chunk, branch)
            for n, (c, pair_of_banks) in enumerate(x_pairs):
                if n > 0:
                    transpose_x(c, 2 * pair_of_banks)
                    transpose_x(c, 2 * pair_of_banks + 1)
                copy_out_x(c, 2 * pair_of_banks)
                copy_out_x(c, 2 * pair_of_banks + 1)
            for chunk, branch in back_at.get(slot, []):
                relu_and_store(chunk, branch)
            for c, g in quant_at.get(slot, []):
                quant_x(c, g)
            if slot == 0:
                regroup_w(4, False)
            if slot == 1:
                quant_w(4)
